import numpy as np
import ml_dtypes


def mxq(x, axis, fmt="e4m3"):
    dtype, down = {"e4m3": (ml_dtypes.float8_e4m3fn, 7), "e5m2": (ml_dtypes.float8_e5m2, 14)}[fmt]
    v = np.moveaxis(np.asarray(x, np.float32).astype(ml_dtypes.bfloat16).astype(np.float64), axis, -1)
    blocks = v.reshape(v.shape[:-1] + (-1, 32))
    amax = np.abs(blocks).max(-1, keepdims=True)
    byte = np.maximum(np.where(amax > 0, np.frexp(amax)[1] - 1 + 127, 0) - down, 1)
    scale = np.exp2(byte - 127.0)
    codes = (blocks / scale).astype(np.float32).astype(dtype).astype(np.float64)
    return np.moveaxis((codes * scale).reshape(v.shape), -1, axis)


WIDE = False


def mx_kscale(k):
    if not WIDE:
        return np.ones(k)
    levels = np.array([10, -10, 5, -5, 0])
    a = np.random.permutation(np.resize(levels, k // 512 * 4)).reshape(k // 512, 4)
    idx = np.arange(k)
    return np.exp2(a[idx // 512, idx % 128 // 32])


BF16 = ml_dtypes.bfloat16


def bf(x):
    return np.asarray(x, np.float32).astype(BF16)


def f64(x):
    return np.asarray(x).astype(np.float64)


B, L, D, C = 32, 20, 8192, 128
EPS = 1e-12


def conv_relu(xq, wq, b):
    k = wq.shape[0]
    n = xq.shape[1]
    out = b
    for j in range(k):
        out = out + (xq[:, j:n - k + 1 + j] @ wq[j])
    return np.maximum(out, 0.0)


def l2norm(x, axis):
    n = np.sqrt(np.sum(x * x, axis=axis, keepdims=True))
    return x / np.maximum(n, EPS)


def setup_inputs():
    s = mx_kscale(D)

    def wdraw(k):
        return bf(np.random.standard_normal((k, D, C)) / np.sqrt(k * D) / s[None, :, None])

    return {"words_emb": bf(np.random.standard_normal((B, L, D)) * s),
            "W1": wdraw(1), "b1": bf(np.random.standard_normal(C) * 0.3),
            "W2": wdraw(2), "b2": bf(np.random.standard_normal(C) * 0.3),
            "W3": wdraw(3), "b3": bf(np.random.standard_normal(C) * 0.3)}


def reference(words_emb, W1, b1, W2, b2, W3, b3):
    xq = mxq(f64(words_emb), 2, "e4m3")
    a = conv_relu(xq, mxq(f64(W1), 1, "e4m3"), f64(b1))
    b_ = conv_relu(xq, mxq(f64(W2), 1, "e4m3"), f64(b2))
    c = conv_relu(xq, mxq(f64(W3), 1, "e4m3"), f64(b3))
    b_pad = np.pad(b_, ((0, 0), (0, L - b_.shape[1]), (0, 0)))
    c_pad = np.pad(c, ((0, 0), (0, L - c.shape[1]), (0, 0)))
    code = np.maximum(np.maximum(a, b_pad), c_pad)
    code = l2norm(code, 2)
    words_out = np.transpose(code, (0, 2, 1))
    pooled = (a.max(axis=1) + b_.max(axis=1) + c.max(axis=1)) / 3.0
    return (words_out, pooled)

@@ -1,0 +1,176 @@
+from contextlib import ExitStack
+
+import concourse.mybir as mybir
+from concourse.masks import make_identity
+
+F32 = mybir.dt.float32
+BF16 = mybir.dt.bfloat16
+U32 = mybir.dt.uint32
+U8 = mybir.dt.uint8
+FP8X4 = mybir.dt.float8_e4m3fn_x4
+ALU = mybir.AluOpType
+ACT = mybir.ActivationFunctionType
+AXIS = mybir.AxisListType
+
+P = 128
+PACK = 4
+K_PASS = P * PACK
+
+SENTENCES, POSITIONS, EMBED, FEATURES = 32, 20, 8192, 128
+TOKENS = SENTENCES * POSITIONS
+PASSES = EMBED // K_PASS
+TOKEN_TILES = TOKENS // P
+MAIN = 512
+REST = TOKENS - MAIN
+
+X_PASSES = 8
+BANK_PASSES = 2
+W_PASSES = 4
+
+FLOPS = 2 * EMBED * FEATURES * SENTENCES * (20 * 1 + 19 * 2 + 18 * 3)
+
+
+def tile_bertheading_pa_k_kernel(tc, words_emb, W1, b1, W2, b2, W3, b3, out_0, out_1):
+    nc = tc.nc
+    x_rows = words_emb.rearrange("n p d -> (n p) d")
+
+    with ExitStack() as stack:
+        keep = stack.enter_context(tc.tile_pool(name="keep", bufs=1))
+        x_pool = stack.enter_context(tc.tile_pool(name="x_pool", bufs=TOKEN_TILES * PASSES // X_PASSES))
+        xg_pool = stack.enter_context(tc.tile_pool(name="xg_pool", bufs=3))
+        w_pool = stack.enter_context(tc.tile_pool(name="w_pool", bufs=4))
+        wq_pool = stack.enter_context(tc.tile_pool(name="wq_pool", bufs=4))
+        sum_pool = stack.enter_context(tc.tile_pool(name="sum_pool", bufs=2))
+        bank_pool = stack.enter_context(tc.psum_pool(name="bank_pool", bufs=4))
+        acc_pool = stack.enter_context(tc.psum_pool(name="acc_pool", bufs=2))
+
+        warm = keep.tile([P, 1], F32)
+        nc.vector.memset(warm[:], 1.0)
+        nc.scalar.activation(out=warm[:], in_=warm[:], func=ACT.Abs_reciprocal_sqrt)
+
+        ident = keep.tile([P, P], F32)
+        make_identity(nc, ident[:])
+        ones = keep.tile([P, P], F32)
+        nc.vector.memset(ones[:], 1.0)
+        code = keep.tile([P, TOKENS], F32)
+        nc.vector.memset(code[:], 0.0)
+        pooled_cn = keep.tile([P, P], F32)
+        nc.vector.memset(pooled_cn[:], 0.0)
+
+        bias_rows = keep.tile([P, P], BF16)
+        nc.vector.memset(bias_rows[:], 0.0)
+        for row, b in enumerate((b1, b2, b3)):
+            nc.scalar.dma_start(out=bias_rows[row : row + 1, :], in_=b.unsqueeze(0))
+
+        x_codes = keep.tile([P, PASSES, TOKENS], U32, align_bytes=64)
+        x_scales = keep.tile([P, PASSES, TOKENS], U8, align_bytes=64)
+        for tt in range(TOKEN_TILES):
+            tokens = slice(tt * P, (tt + 1) * P)
+            for half in range(PASSES // X_PASSES):
+                x_raw = x_pool.tile([P, X_PASSES * K_PASS], BF16)
+                nc.sync.dma_start(
+                    out=x_raw[:], in_=x_rows[tokens, half * X_PASSES * K_PASS : (half + 1) * X_PASSES * K_PASS]
+                )
+                x_words = x_raw[:].bitcast(F32).rearrange("r (g p u) -> r g u p", p=P, u=2)
+                x_grouped = xg_pool.tile([P, X_PASSES * P * PACK], BF16, align_bytes=64)
+                x_grouped_words = x_grouped[:].bitcast(F32).rearrange("p (g r u) -> p g r u", r=P, u=2)
+                for bank_no in range(X_PASSES // BANK_PASSES):
+                    first = bank_no * BANK_PASSES
+                    bank = bank_pool.tile([P, BANK_PASSES, 2, P], F32, tag="bank")
+                    for g in range(BANK_PASSES):
+                        for u in range(2):
+                            nc.tensor.transpose(bank[:, g, u, :], x_words[:, first + g, u, :], ident[:])
+                    copy_out = nc.vector.tensor_copy if bank_no % 4 == 3 else nc.scalar.copy
+                    copy_out(
+                        out=x_grouped_words[:, first : first + BANK_PASSES, :, :],
+                        in_=bank[:].rearrange("p g u r -> p g r u"),
+                    )
+                for g in range(X_PASSES):
+                    nc.vector.quantize_mx(
+                        out=x_codes[:, half * X_PASSES + g, tokens].bitcast(FP8X4),
+                        scales=x_scales[:, half * X_PASSES + g, tokens],
+                        in_=x_grouped[:, g * P * PACK : (g + 1) * P * PACK],
+                    )
+
+        bias_rows_f32 = keep.tile([P, P], F32)
+        nc.vector.tensor_copy(out=bias_rows_f32[:], in_=bias_rows[:])
+        bias_bank = bank_pool.tile([P, P], F32, tag="bank")
+        nc.tensor.transpose(bias_bank[:], bias_rows_f32[:], ident[:])
+        bias = keep.tile([P, 3], F32)
+        nc.vector.tensor_copy(out=bias[:], in_=bias_bank[:, 0:3])
+
+        peak = keep.tile([P, 3, SENTENCES], F32)
+        code_np = code[:].rearrange("c (n p) -> c n p", p=POSITIONS)
+        chunk_no = 0
+        for width, w in ((3, W3), (2, W2), (1, W1)):
+            conv = sum_pool.tile([P, TOKENS], F32)
+            for tap in range(width):
+                acc_main = acc_pool.tile([P, MAIN], F32)
+                acc_rest = acc_pool.tile([P, REST], F32)
+                for chunk in range(PASSES // W_PASSES):
+                    rows = slice(chunk * W_PASSES * K_PASS, (chunk + 1) * W_PASSES * K_PASS)
+                    w_raw = w_pool.tile([P, W_PASSES, PACK, FEATURES], BF16)
+                    nc.sync.dma_start(out=w_raw[:], in_=w[tap, rows, :].rearrange("(g p t) c -> p g t c", p=P, t=PACK))
+                    w_grouped = w_pool.tile([P, W_PASSES, FEATURES, PACK], BF16, align_bytes=64)
+                    regroup = nc.vector.tensor_copy if chunk_no % 2 == 0 else nc.scalar.copy
+                    regroup(out=w_grouped[:], in_=w_raw[:].rearrange("p g t c -> p g c t"))
+                    chunk_no += 1
+                    w_codes = wq_pool.tile([P, W_PASSES * FEATURES], U32, align_bytes=64)
+                    w_scales = wq_pool.tile([P, W_PASSES * FEATURES], U8, align_bytes=64)
+                    nc.vector.quantize_mx(
+                        out=w_codes[:].bitcast(FP8X4),
+                        scales=w_scales[:],
+                        in_=w_grouped[:].rearrange("p g c t -> p (g c t)"),
+                    )
+                    for g in range(W_PASSES):
+                        k_pass = chunk * W_PASSES + g
+                        cols = slice(g * FEATURES, (g + 1) * FEATURES)
+                        for acc, toks in ((acc_main, slice(0, MAIN)), (acc_rest, slice(MAIN, TOKENS))):
+                            nc.tensor.matmul_mx(
+                                out=acc[:],
+                                lhsT=w_codes[:, cols].bitcast(FP8X4),
+                                lhsT_scale=w_scales[:, cols],
+                                rhs=x_codes[:, k_pass, toks].bitcast(FP8X4),
+                                rhs_scale=x_scales[:, k_pass, toks],
+                                start=(k_pass == 0),
+                                stop=(k_pass == PASSES - 1),
+                            )
+                if tap == 0:
+                    b_col = bias[:, width - 1 : width]
+                    nc.scalar.activation(out=conv[:, 0:MAIN], in_=acc_main[:], func=ACT.Identity, bias=b_col)
+                    nc.scalar.activation(out=conv[:, MAIN:TOKENS], in_=acc_rest[:], func=ACT.Identity, bias=b_col)
+                else:
+                    low = conv[:, 0 : MAIN - tap]
+                    high = conv[:, MAIN - tap : TOKENS - tap]
+                    nc.vector.tensor_tensor(out=low, in0=low, in1=acc_main[:, tap:MAIN], op=ALU.add)
+                    nc.vector.tensor_tensor(out=high, in0=high, in1=acc_rest[:], op=ALU.add)
+            own = POSITIONS - width + 1
+            conv_np = conv[:].rearrange("c (n p) -> c n p", p=POSITIONS)[:, :, 0:own]
+            nc.vector.tensor_tensor(out=code_np[:, :, 0:own], in0=code_np[:, :, 0:own], in1=conv_np, op=ALU.max)
+            nc.vector.tensor_reduce(out=peak[:, width - 1, :], in_=conv_np, axis=AXIS.X, op=ALU.max)
+
+        squares = keep.tile([P, TOKENS], F32)
+        nc.scalar.activation(out=squares[:], in_=code[:], func=ACT.Square)
+        inv_norm = keep.tile([P, TOKENS], F32)
+        for lo, hi in ((0, MAIN), (MAIN, TOKENS)):
+            norm_bank = bank_pool.tile([P, hi - lo], F32, tag="bank")
+            nc.tensor.matmul(out=norm_bank[:], lhsT=ones[:], rhs=squares[:, lo:hi], start=True, stop=True)
+            nc.scalar.activation(out=inv_norm[:, lo:hi], in_=norm_bank[:], func=ACT.Abs_reciprocal_sqrt)
+        words = keep.tile([P, TOKENS], F32)
+        nc.vector.scalar_tensor_tensor(
+            out=words[:], in0=inv_norm[:], scalar=1.0e12, in1=code[:], op0=ALU.min, op1=ALU.mult
+        )
+        with nc.allow_non_contiguous_dma(reason="a feature's 20 positions of one sentence are an 80-byte run"):
+            nc.sync.dma_start(
+                out=out_0.rearrange("n c p -> c n p"), in_=words[:].rearrange("c (n p) -> c n p", p=POSITIONS)
+            )
+
+        nc.vector.tensor_scalar_max(out=peak[:], in0=peak[:], scalar1=0.0)
+        nc.vector.tensor_reduce(
+            out=pooled_cn[:, 0:SENTENCES], in_=peak[:].rearrange("c k n -> c n k"), axis=AXIS.X, op=ALU.add
+        )
+        pooled_bank = bank_pool.tile([P, P], F32, tag="bank")
+        nc.tensor.transpose(pooled_bank[:], pooled_cn[:], ident[:])
+        pooled_nc = keep.tile([P, FEATURES], F32)
+        nc.scalar.activation(out=pooled_nc[:], in_=pooled_bank[:], func=ACT.Copy, scale=1.0 / 3.0)
+        nc.scalar.dma_start(out=out_1, in_=pooled_nc[0:SENTENCES, :])

@@ -23,9 +23,14 @@ TOKEN_TILES = TOKENS // P
 MAIN = 512
 REST = TOKENS - MAIN
 
-X_PASSES = 8
+CHUNK_PASSES = 4
+CHUNK = CHUNK_PASSES * K_PASS
+PARTS = PASSES // CHUNK_PASSES
 BANK_PASSES = 2
-W_PASSES = 4
+W_AHEAD = 6
+TAP_LAG = 2
+PIECE = 8
+PIECE_TOKENS = PIECE * POSITIONS
 
 FLOPS = 2 * EMBED * FEATURES * SENTENCES * (20 * 1 + 19 * 2 + 18 * 3)
 
@@ -35,10 +40,12 @@ def tile_bertheading_pa_k_kernel(tc, words_emb, W1, b1, W2, b2, W3, b3, out_0, o
     x_rows = words_emb.rearrange("n p d -> (n p) d")
 
     with ExitStack() as stack:
+        stack.enter_context(tc.manual_schedule())
         keep = stack.enter_context(tc.tile_pool(name="keep", bufs=1))
-        x_pool = stack.enter_context(tc.tile_pool(name="x_pool", bufs=TOKEN_TILES * PASSES // X_PASSES))
-        xg_pool = stack.enter_context(tc.tile_pool(name="xg_pool", bufs=3))
-        w_pool = stack.enter_context(tc.tile_pool(name="w_pool", bufs=4))
+        x_pool = stack.enter_context(tc.tile_pool(name="x_pool", bufs=TOKEN_TILES * PARTS))
+        xg_pool = stack.enter_context(tc.tile_pool(name="xg_pool", bufs=4))
+        w_pool = stack.enter_context(tc.tile_pool(name="w_pool", bufs=W_AHEAD))
+        wg_pool = stack.enter_context(tc.tile_pool(name="wg_pool", bufs=3))
         wq_pool = stack.enter_context(tc.tile_pool(name="wq_pool", bufs=4))
         sum_pool = stack.enter_context(tc.tile_pool(name="sum_pool", bufs=2))
         bank_pool = stack.enter_context(tc.psum_pool(name="bank_pool", bufs=4))
@@ -56,41 +63,69 @@ def tile_bertheading_pa_k_kernel(tc, words_emb, W1, b1, W2, b2, W3, b3, out_0, o
         nc.vector.memset(code[:], 0.0)
         pooled_cn = keep.tile([P, P], F32)
         nc.vector.memset(pooled_cn[:], 0.0)
-
         bias_rows = keep.tile([P, P], BF16)
         nc.vector.memset(bias_rows[:], 0.0)
         for row, b in enumerate((b1, b2, b3)):
             nc.scalar.dma_start(out=bias_rows[row : row + 1, :], in_=b.unsqueeze(0))
 
+        x_pieces = [(part, tt) for part in range(PARTS) for tt in range(TOKEN_TILES)]
+        x_raw = {}
+        for i, (part, tt) in enumerate(x_pieces):
+            x_raw[i] = x_pool.tile([P, CHUNK], BF16, name="x_raw")
+            nc.sync.dma_start(out=x_raw[i][:], in_=x_rows[tt * P : (tt + 1) * P, part * CHUNK : (part + 1) * CHUNK])
+
+        chunks = [
+            (width, w, tap, part)
+            for width, w in ((3, W3), (2, W2), (1, W1))
+            for tap in range(width)
+            for part in range(PARTS)
+        ]
+        w_raw, w_grouped, w_codes, w_scales = {}, {}, {}, {}
+
+        def load(i):
+            width, w, tap, part = chunks[i]
+            w_raw[i] = w_pool.tile([P, CHUNK_PASSES, PACK, FEATURES], BF16, name="w_raw")
+            rows = w[tap, part * CHUNK : (part + 1) * CHUNK, :]
+            nc.sync.dma_start(out=w_raw[i][:], in_=rows.rearrange("(g p t) c -> p g t c", p=P, t=PACK))
+
+        for i in range(W_AHEAD):
+            load(i)
+
         x_codes = keep.tile([P, PASSES, TOKENS], U32, align_bytes=64)
         x_scales = keep.tile([P, PASSES, TOKENS], U8, align_bytes=64)
-        for tt in range(TOKEN_TILES):
-            tokens = slice(tt * P, (tt + 1) * P)
-            for half in range(PASSES // X_PASSES):
-                x_raw = x_pool.tile([P, X_PASSES * K_PASS], BF16)
-                nc.sync.dma_start(
-                    out=x_raw[:], in_=x_rows[tokens, half * X_PASSES * K_PASS : (half + 1) * X_PASSES * K_PASS]
+        x_grouped = {}
+
+        def transpose_x(i):
+            x_words = x_raw[i][:].bitcast(F32).rearrange("r (g p u) -> r g u p", p=P, u=2)
+            x_grouped[i] = xg_pool.tile([P, CHUNK_PASSES * P * PACK], BF16, name="x_grouped", align_bytes=64)
+            grouped_words = x_grouped[i][:].bitcast(F32).rearrange("p (g r u) -> p g r u", r=P, u=2)
+            for j in range(CHUNK_PASSES // BANK_PASSES):
+                first = j * BANK_PASSES
+                bank = bank_pool.tile([P, BANK_PASSES, 2, P], F32, tag="bank")
+                for g in range(BANK_PASSES):
+                    for u in range(2):
+                        nc.tensor.transpose(bank[:, g, u, :], x_words[:, first + g, u, :], ident[:])
+                bank_no = i * (CHUNK_PASSES // BANK_PASSES) + j
+                copy_out = nc.vector.tensor_copy if bank_no % 4 == 3 else nc.scalar.copy
+                copy_out(
+                    out=grouped_words[:, first : first + BANK_PASSES, :, :],
+                    in_=bank[:].rearrange("p g u r -> p g r u"),
                 )
-                x_words = x_raw[:].bitcast(F32).rearrange("r (g p u) -> r g u p", p=P, u=2)
-                x_grouped = xg_pool.tile([P, X_PASSES * P * PACK], BF16, align_bytes=64)
-                x_grouped_words = x_grouped[:].bitcast(F32).rearrange("p (g r u) -> p g r u", r=P, u=2)
-                for bank_no in range(X_PASSES // BANK_PASSES):
-                    first = bank_no * BANK_PASSES
-                    bank = bank_pool.tile([P, BANK_PASSES, 2, P], F32, tag="bank")
-                    for g in range(BANK_PASSES):
-                        for u in range(2):
-                            nc.tensor.transpose(bank[:, g, u, :], x_words[:, first + g, u, :], ident[:])
-                    copy_out = nc.vector.tensor_copy if bank_no % 4 == 3 else nc.scalar.copy
-                    copy_out(
-                        out=x_grouped_words[:, first : first + BANK_PASSES, :, :],
-                        in_=bank[:].rearrange("p g u r -> p g r u"),
-                    )
-                for g in range(X_PASSES):
-                    nc.vector.quantize_mx(
-                        out=x_codes[:, half * X_PASSES + g, tokens].bitcast(FP8X4),
-                        scales=x_scales[:, half * X_PASSES + g, tokens],
-                        in_=x_grouped[:, g * P * PACK : (g + 1) * P * PACK],
-                    )
+
+        def quantise_x(i):
+            part, tt = x_pieces[i]
+            for g in range(CHUNK_PASSES):
+                nc.vector.quantize_mx(
+                    out=x_codes[:, part * CHUNK_PASSES + g, tt * P : (tt + 1) * P].bitcast(FP8X4),
+                    scales=x_scales[:, part * CHUNK_PASSES + g, tt * P : (tt + 1) * P],
+                    in_=x_grouped[i][:, g * P * PACK : (g + 1) * P * PACK],
+                )
+
+        for step in range(len(x_pieces) + 1):
+            if step < len(x_pieces):
+                transpose_x(step)
+            if step >= 1:
+                quantise_x(step - 1)
 
         bias_rows_f32 = keep.tile([P, P], F32)
         nc.vector.tensor_copy(out=bias_rows_f32[:], in_=bias_rows[:])
@@ -99,76 +134,137 @@ def tile_bertheading_pa_k_kernel(tc, words_emb, W1, b1, W2, b2, W3, b3, out_0, o
         bias = keep.tile([P, 3], F32)
         nc.vector.tensor_copy(out=bias[:], in_=bias_bank[:, 0:3])
 
+        acc, conv = {}, {}
         peak = keep.tile([P, 3, SENTENCES], F32)
         code_np = code[:].rearrange("c (n p) -> c n p", p=POSITIONS)
-        chunk_no = 0
-        for width, w in ((3, W3), (2, W2), (1, W1)):
-            conv = sum_pool.tile([P, TOKENS], F32)
-            for tap in range(width):
-                acc_main = acc_pool.tile([P, MAIN], F32)
-                acc_rest = acc_pool.tile([P, REST], F32)
-                for chunk in range(PASSES // W_PASSES):
-                    rows = slice(chunk * W_PASSES * K_PASS, (chunk + 1) * W_PASSES * K_PASS)
-                    w_raw = w_pool.tile([P, W_PASSES, PACK, FEATURES], BF16)
-                    nc.sync.dma_start(out=w_raw[:], in_=w[tap, rows, :].rearrange("(g p t) c -> p g t c", p=P, t=PACK))
-                    w_grouped = w_pool.tile([P, W_PASSES, FEATURES, PACK], BF16, align_bytes=64)
-                    regroup = nc.vector.tensor_copy if chunk_no % 2 == 0 else nc.scalar.copy
-                    regroup(out=w_grouped[:], in_=w_raw[:].rearrange("p g t c -> p g c t"))
-                    chunk_no += 1
-                    w_codes = wq_pool.tile([P, W_PASSES * FEATURES], U32, align_bytes=64)
-                    w_scales = wq_pool.tile([P, W_PASSES * FEATURES], U8, align_bytes=64)
-                    nc.vector.quantize_mx(
-                        out=w_codes[:].bitcast(FP8X4),
-                        scales=w_scales[:],
-                        in_=w_grouped[:].rearrange("p g c t -> p (g c t)"),
-                    )
-                    for g in range(W_PASSES):
-                        k_pass = chunk * W_PASSES + g
-                        cols = slice(g * FEATURES, (g + 1) * FEATURES)
-                        for acc, toks in ((acc_main, slice(0, MAIN)), (acc_rest, slice(MAIN, TOKENS))):
-                            nc.tensor.matmul_mx(
-                                out=acc[:],
-                                lhsT=w_codes[:, cols].bitcast(FP8X4),
-                                lhsT_scale=w_scales[:, cols],
-                                rhs=x_codes[:, k_pass, toks].bitcast(FP8X4),
-                                rhs_scale=x_scales[:, k_pass, toks],
-                                start=(k_pass == 0),
-                                stop=(k_pass == PASSES - 1),
-                            )
-                if tap == 0:
-                    b_col = bias[:, width - 1 : width]
-                    nc.scalar.activation(out=conv[:, 0:MAIN], in_=acc_main[:], func=ACT.Identity, bias=b_col)
-                    nc.scalar.activation(out=conv[:, MAIN:TOKENS], in_=acc_rest[:], func=ACT.Identity, bias=b_col)
-                else:
-                    low = conv[:, 0 : MAIN - tap]
-                    high = conv[:, MAIN - tap : TOKENS - tap]
-                    nc.vector.tensor_tensor(out=low, in0=low, in1=acc_main[:, tap:MAIN], op=ALU.add)
-                    nc.vector.tensor_tensor(out=high, in0=high, in1=acc_rest[:], op=ALU.add)
-            own = POSITIONS - width + 1
-            conv_np = conv[:].rearrange("c (n p) -> c n p", p=POSITIONS)[:, :, 0:own]
-            nc.vector.tensor_tensor(out=code_np[:, :, 0:own], in0=code_np[:, :, 0:own], in1=conv_np, op=ALU.max)
-            nc.vector.tensor_reduce(out=peak[:, width - 1, :], in_=conv_np, axis=AXIS.X, op=ALU.max)
 
-        squares = keep.tile([P, TOKENS], F32)
-        nc.scalar.activation(out=squares[:], in_=code[:], func=ACT.Square)
-        inv_norm = keep.tile([P, TOKENS], F32)
-        for lo, hi in ((0, MAIN), (MAIN, TOKENS)):
-            norm_bank = bank_pool.tile([P, hi - lo], F32, tag="bank")
-            nc.tensor.matmul(out=norm_bank[:], lhsT=ones[:], rhs=squares[:, lo:hi], start=True, stop=True)
-            nc.scalar.activation(out=inv_norm[:, lo:hi], in_=norm_bank[:], func=ACT.Abs_reciprocal_sqrt)
-        words = keep.tile([P, TOKENS], F32)
-        nc.vector.scalar_tensor_tensor(
-            out=words[:], in0=inv_norm[:], scalar=1.0e12, in1=code[:], op0=ALU.min, op1=ALU.mult
-        )
-        with nc.allow_non_contiguous_dma(reason="a feature's 20 positions of one sentence are an 80-byte run"):
-            nc.sync.dma_start(
-                out=out_0.rearrange("n c p -> c n p"), in_=words[:].rearrange("c (n p) -> c n p", p=POSITIONS)
+        def regroup(i):
+            w_grouped[i] = wg_pool.tile([P, CHUNK_PASSES, FEATURES, PACK], BF16, name="w_grouped", align_bytes=64)
+            if i % 2 == 0:
+                nc.vector.tensor_copy(
+                    out=w_grouped[i][:].rearrange("p g (c i) t -> p g c t i", i=4),
+                    in_=w_raw[i][:].rearrange("p g t (c i) -> p g c t i", i=4),
+                )
+            else:
+                for g in range(CHUNK_PASSES):
+                    nc.scalar.copy(
+                        out=w_grouped[i][:, g].rearrange("p (c i) t -> p c t i", i=4),
+                        in_=w_raw[i][:, g].rearrange("p t (c i) -> p c t i", i=4),
+                    )
+
+        def quantise(i):
+            w_codes[i] = wq_pool.tile([P, CHUNK_PASSES * FEATURES], U32, name="w_codes", align_bytes=64)
+            w_scales[i] = wq_pool.tile([P, CHUNK_PASSES * FEATURES], U8, name="w_scales", align_bytes=64)
+            nc.vector.quantize_mx(
+                out=w_codes[i][:].bitcast(FP8X4),
+                scales=w_scales[i][:],
+                in_=w_grouped[i][:].rearrange("p g c t -> p (g c t)"),
             )
 
+        def multiply(i):
+            part = i % PARTS
+            if part == 0:
+                acc_main = acc_pool.tile([P, MAIN], F32)
+                acc_rest = acc_pool.tile([P, REST], F32)
+                acc[i // PARTS] = (acc_main, acc_rest)
+            for g in range(CHUNK_PASSES):
+                k_pass = part * CHUNK_PASSES + g
+                cols = slice(g * FEATURES, (g + 1) * FEATURES)
+                for bank, toks in zip(acc[i // PARTS], (slice(0, MAIN), slice(MAIN, TOKENS))):
+                    nc.tensor.matmul_mx(
+                        out=bank[:],
+                        lhsT=w_codes[i][:, cols].bitcast(FP8X4),
+                        lhsT_scale=w_scales[i][:, cols],
+                        rhs=x_codes[:, k_pass, toks].bitcast(FP8X4),
+                        rhs_scale=x_scales[:, k_pass, toks],
+                        start=(k_pass == 0),
+                        stop=(k_pass == PASSES - 1),
+                    )
+
+        def add_tap(tap_no, lo, hi):
+            width, w, tap, part = chunks[tap_no * PARTS]
+            hi = min(hi, TOKENS - tap)
+            cut = min(max(MAIN - tap, lo), hi)
+            for bank, dst_lo, dst_hi, src_lo in ((0, lo, cut, lo + tap), (1, cut, hi, cut + tap - MAIN)):
+                if dst_lo < dst_hi:
+                    dst = conv[width][:, dst_lo:dst_hi]
+                    product = acc[tap_no][bank][:, src_lo : src_lo + dst_hi - dst_lo]
+                    if tap == 0:
+                        nc.scalar.activation(out=dst, in_=product, func=ACT.Identity, bias=bias[:, width - 1 : width])
+                    else:
+                        nc.vector.tensor_tensor(out=dst, in0=dst, in1=product, op=ALU.add)
+
+        def own_positions(width, n_lo, n_hi):
+            own = POSITIONS - width + 1
+            conv_np = conv[width][:].rearrange("c (n p) -> c n p", p=POSITIONS)
+            return code_np[:, n_lo:n_hi, 0:own], conv_np[:, n_lo:n_hi, 0:own]
+
+        def raise_code(width, n_lo, n_hi):
+            code_own, conv_own = own_positions(width, n_lo, n_hi)
+            nc.vector.tensor_tensor(out=code_own, in0=code_own, in1=conv_own, op=ALU.max)
+
+        def take_peak(width):
+            code_own, conv_own = own_positions(width, 0, SENTENCES)
+            nc.vector.tensor_reduce(out=peak[:, width - 1, :], in_=conv_own, axis=AXIS.X, op=ALU.max)
+
+        last_tap = len(chunks) // PARTS - 1
+        for step in range(len(chunks) + 2):
+            if step < len(chunks):
+                regroup(step)
+            if step + W_AHEAD < len(chunks):
+                load(step + W_AHEAD)
+            if 1 <= step <= len(chunks):
+                quantise(step - 1)
+            if step >= 2:
+                multiply(step - 2)
+            closed = step - 2 - TAP_LAG
+            if closed >= 0 and closed % PARTS == PARTS - 1 and closed // PARTS < last_tap:
+                width, w, tap, part = chunks[closed]
+                if tap == 0:
+                    conv[width] = sum_pool.tile([P, TOKENS], F32, name="conv")
+                add_tap(closed // PARTS, 0, TOKENS)
+                if tap == width - 1:
+                    raise_code(width, 0, SENTENCES)
+                    take_peak(width)
+
+        pieces = range(SENTENCES // PIECE)
+        conv[1] = sum_pool.tile([P, TOKENS], F32, name="conv")
+        squares = keep.tile([P, TOKENS], F32)
+        inv_norm = keep.tile([P, TOKENS], F32)
+        words = keep.tile([P, TOKENS], F32)
+        norm_bank = {}
+        for i in pieces:
+            add_tap(last_tap, i * PIECE_TOKENS, (i + 1) * PIECE_TOKENS)
+        for i in pieces:
+            raise_code(1, i * PIECE, (i + 1) * PIECE)
+        for i in pieces:
+            toks = slice(i * PIECE_TOKENS, (i + 1) * PIECE_TOKENS)
+            nc.scalar.activation(out=squares[:, toks], in_=code[:, toks], func=ACT.Square)
+        for i in pieces:
+            toks = slice(i * PIECE_TOKENS, (i + 1) * PIECE_TOKENS)
+            norm_bank[i] = bank_pool.tile([P, PIECE_TOKENS], F32, name="norm_bank", tag="bank")
+            nc.tensor.matmul(out=norm_bank[i][:], lhsT=ones[:], rhs=squares[:, toks], start=True, stop=True)
+
+        take_peak(1)
         nc.vector.tensor_scalar_max(out=peak[:], in0=peak[:], scalar1=0.0)
         nc.vector.tensor_reduce(
             out=pooled_cn[:, 0:SENTENCES], in_=peak[:].rearrange("c k n -> c n k"), axis=AXIS.X, op=ALU.add
         )
+
+        for i in pieces:
+            toks = slice(i * PIECE_TOKENS, (i + 1) * PIECE_TOKENS)
+            nc.scalar.activation(out=inv_norm[:, toks], in_=norm_bank[i][:], func=ACT.Abs_reciprocal_sqrt)
+        with nc.allow_non_contiguous_dma(reason="a feature's 20 positions of one sentence are an 80-byte run"):
+            for i in pieces:
+                toks = slice(i * PIECE_TOKENS, (i + 1) * PIECE_TOKENS)
+                nc.vector.scalar_tensor_tensor(
+                    out=words[:, toks], in0=inv_norm[:, toks], scalar=1.0e12, in1=code[:, toks], op0=ALU.min, op1=ALU.mult
+                )
+                nc.sync.dma_start(
+                    out=out_0[i * PIECE : (i + 1) * PIECE].rearrange("n c p -> c n p"),
+                    in_=words[:, toks].rearrange("c (n p) -> c n p", p=POSITIONS),
+                )
+
         pooled_bank = bank_pool.tile([P, P], F32, tag="bank")
         nc.tensor.transpose(pooled_bank[:], pooled_cn[:], ident[:])
         pooled_nc = keep.tile([P, FEATURES], F32)

@@ -23,27 +23,28 @@ TOKEN_TILES = TOKENS // P
 MAIN = 512
 REST = TOKENS - MAIN
 
+TILE_POSITIONS = P // SENTENCES
+X_PASSES = 8
+X_PIECE = X_PASSES * K_PASS
+BANK_PASSES = 2
 CHUNK_PASSES = 4
 CHUNK = CHUNK_PASSES * K_PASS
 PARTS = PASSES // CHUNK_PASSES
-BANK_PASSES = 2
 W_AHEAD = 6
 TAP_LAG = 2
-PIECE = 8
-PIECE_TOKENS = PIECE * POSITIONS
+BLOCK = 32
 
 FLOPS = 2 * EMBED * FEATURES * SENTENCES * (20 * 1 + 19 * 2 + 18 * 3)
 
 
 def tile_bertheading_pa_k_kernel(tc, words_emb, W1, b1, W2, b2, W3, b3, out_0, out_1):
     nc = tc.nc
-    x_rows = words_emb.rearrange("n p d -> (n p) d")
 
     with ExitStack() as stack:
         stack.enter_context(tc.manual_schedule())
         keep = stack.enter_context(tc.tile_pool(name="keep", bufs=1))
-        x_pool = stack.enter_context(tc.tile_pool(name="x_pool", bufs=TOKEN_TILES * PARTS))
-        xg_pool = stack.enter_context(tc.tile_pool(name="xg_pool", bufs=4))
+        x_pool = stack.enter_context(tc.tile_pool(name="x_pool", bufs=TOKEN_TILES * PASSES // X_PASSES))
+        xg_pool = stack.enter_context(tc.tile_pool(name="xg_pool", bufs=3))
         w_pool = stack.enter_context(tc.tile_pool(name="w_pool", bufs=W_AHEAD))
         wg_pool = stack.enter_context(tc.tile_pool(name="wg_pool", bufs=3))
         wq_pool = stack.enter_context(tc.tile_pool(name="wq_pool", bufs=4))
@@ -57,22 +58,36 @@ def tile_bertheading_pa_k_kernel(tc, words_emb, W1, b1, W2, b2, W3, b3, out_0, o
 
         ident = keep.tile([P, P], F32)
         make_identity(nc, ident[:])
-        ones = keep.tile([P, P], F32)
-        nc.vector.memset(ones[:], 1.0)
-        code = keep.tile([P, TOKENS], F32)
+        code = keep.tile([P, TOKENS], F32, align_bytes=64)
         nc.vector.memset(code[:], 0.0)
-        pooled_cn = keep.tile([P, P], F32)
-        nc.vector.memset(pooled_cn[:], 0.0)
         bias_rows = keep.tile([P, P], BF16)
         nc.vector.memset(bias_rows[:], 0.0)
         for row, b in enumerate((b1, b2, b3)):
             nc.scalar.dma_start(out=bias_rows[row : row + 1, :], in_=b.unsqueeze(0))
 
-        x_pieces = [(part, tt) for part in range(PARTS) for tt in range(TOKEN_TILES)]
+        perm = keep.tile([P, P], F32)
+        nc.vector.tensor_copy(
+            out=perm[:].rearrange("i (a n) -> i a n", n=SENTENCES), in_=ident[:].rearrange("i (n a) -> i a n", n=SENTENCES)
+        )
+        fold_column = keep.tile([P, BLOCK], F32)
+        nc.vector.tensor_reduce(
+            out=fold_column[:], in_=ident[:].rearrange("i (b n) -> i n b", n=BLOCK), axis=AXIS.X, op=ALU.add
+        )
+        fold = keep.tile([P, P], F32)
+        nc.vector.tensor_copy(
+            out=fold[:].rearrange("i (b n) -> i b n", n=BLOCK),
+            in_=fold_column[:].unsqueeze(1).to_broadcast([P, P // BLOCK, BLOCK]),
+        )
+
+        x_pieces = [(half, tt) for half in range(PASSES // X_PASSES) for tt in range(TOKEN_TILES)]
         x_raw = {}
-        for i, (part, tt) in enumerate(x_pieces):
-            x_raw[i] = x_pool.tile([P, CHUNK], BF16, name="x_raw")
-            nc.sync.dma_start(out=x_raw[i][:], in_=x_rows[tt * P : (tt + 1) * P, part * CHUNK : (part + 1) * CHUNK])
+        for i, (half, tt) in enumerate(x_pieces):
+            x_raw[i] = x_pool.tile([P, X_PIECE], BF16, name="x_raw")
+            for a in range(TILE_POSITIONS):
+                nc.sync.dma_start(
+                    out=x_raw[i][a:P:TILE_POSITIONS, :],
+                    in_=words_emb[:, tt * TILE_POSITIONS + a, half * X_PIECE : (half + 1) * X_PIECE],
+                )
 
         chunks = [
             (width, w, tap, part)
@@ -97,27 +112,26 @@ def tile_bertheading_pa_k_kernel(tc, words_emb, W1, b1, W2, b2, W3, b3, out_0, o
 
         def transpose_x(i):
             x_words = x_raw[i][:].bitcast(F32).rearrange("r (g p u) -> r g u p", p=P, u=2)
-            x_grouped[i] = xg_pool.tile([P, CHUNK_PASSES * P * PACK], BF16, name="x_grouped", align_bytes=64)
+            x_grouped[i] = xg_pool.tile([P, X_PASSES * P * PACK], BF16, name="x_grouped", align_bytes=64)
             grouped_words = x_grouped[i][:].bitcast(F32).rearrange("p (g r u) -> p g r u", r=P, u=2)
-            for j in range(CHUNK_PASSES // BANK_PASSES):
+            for j in range(X_PASSES // BANK_PASSES):
                 first = j * BANK_PASSES
                 bank = bank_pool.tile([P, BANK_PASSES, 2, P], F32, tag="bank")
                 for g in range(BANK_PASSES):
                     for u in range(2):
-                        nc.tensor.transpose(bank[:, g, u, :], x_words[:, first + g, u, :], ident[:])
-                bank_no = i * (CHUNK_PASSES // BANK_PASSES) + j
-                copy_out = nc.vector.tensor_copy if bank_no % 4 == 3 else nc.scalar.copy
+                        nc.tensor.transpose(bank[:, g, u, :], x_words[:, first + g, u, :], perm[:])
+                copy_out = nc.vector.tensor_copy if j % 4 == 3 else nc.scalar.copy
                 copy_out(
                     out=grouped_words[:, first : first + BANK_PASSES, :, :],
                     in_=bank[:].rearrange("p g u r -> p g r u"),
                 )
 
         def quantise_x(i):
-            part, tt = x_pieces[i]
-            for g in range(CHUNK_PASSES):
+            half, tt = x_pieces[i]
+            for g in range(X_PASSES):
                 nc.vector.quantize_mx(
-                    out=x_codes[:, part * CHUNK_PASSES + g, tt * P : (tt + 1) * P].bitcast(FP8X4),
-                    scales=x_scales[:, part * CHUNK_PASSES + g, tt * P : (tt + 1) * P],
+                    out=x_codes[:, half * X_PASSES + g, tt * P : (tt + 1) * P].bitcast(FP8X4),
+                    scales=x_scales[:, half * X_PASSES + g, tt * P : (tt + 1) * P],
                     in_=x_grouped[i][:, g * P * PACK : (g + 1) * P * PACK],
                 )
 
@@ -136,7 +150,6 @@ def tile_bertheading_pa_k_kernel(tc, words_emb, W1, b1, W2, b2, W3, b3, out_0, o
 
         acc, conv = {}, {}
         peak = keep.tile([P, 3, SENTENCES], F32)
-        code_np = code[:].rearrange("c (n p) -> c n p", p=POSITIONS)
 
         def regroup(i):
             w_grouped[i] = wg_pool.tile([P, CHUNK_PASSES, FEATURES, PACK], BF16, name="w_grouped", align_bytes=64)
@@ -181,11 +194,14 @@ def tile_bertheading_pa_k_kernel(tc, words_emb, W1, b1, W2, b2, W3, b3, out_0, o
                         stop=(k_pass == PASSES - 1),
                     )
 
+        def own_tokens(width):
+            return (POSITIONS - width + 1) * SENTENCES
+
         def add_tap(tap_no, lo, hi):
             width, w, tap, part = chunks[tap_no * PARTS]
-            hi = min(hi, TOKENS - tap)
-            cut = min(max(MAIN - tap, lo), hi)
-            for bank, dst_lo, dst_hi, src_lo in ((0, lo, cut, lo + tap), (1, cut, hi, cut + tap - MAIN)):
+            shift = tap * SENTENCES
+            cut = min(max(MAIN - shift, lo), hi)
+            for bank, dst_lo, dst_hi, src_lo in ((0, lo, cut, lo + shift), (1, cut, hi, cut + shift - MAIN)):
                 if dst_lo < dst_hi:
                     dst = conv[width][:, dst_lo:dst_hi]
                     product = acc[tap_no][bank][:, src_lo : src_lo + dst_hi - dst_lo]
@@ -194,18 +210,12 @@ def tile_bertheading_pa_k_kernel(tc, words_emb, W1, b1, W2, b2, W3, b3, out_0, o
                     else:
                         nc.vector.tensor_tensor(out=dst, in0=dst, in1=product, op=ALU.add)
 
-        def own_positions(width, n_lo, n_hi):
-            own = POSITIONS - width + 1
-            conv_np = conv[width][:].rearrange("c (n p) -> c n p", p=POSITIONS)
-            return code_np[:, n_lo:n_hi, 0:own], conv_np[:, n_lo:n_hi, 0:own]
-
-        def raise_code(width, n_lo, n_hi):
-            code_own, conv_own = own_positions(width, n_lo, n_hi)
-            nc.vector.tensor_tensor(out=code_own, in0=code_own, in1=conv_own, op=ALU.max)
+        def raise_code(width, lo, hi):
+            nc.vector.tensor_tensor(out=code[:, lo:hi], in0=code[:, lo:hi], in1=conv[width][:, lo:hi], op=ALU.max)
 
         def take_peak(width):
-            code_own, conv_own = own_positions(width, 0, SENTENCES)
-            nc.vector.tensor_reduce(out=peak[:, width - 1, :], in_=conv_own, axis=AXIS.X, op=ALU.max)
+            own = conv[width][:, 0 : own_tokens(width)].rearrange("c (p n) -> c n p", n=SENTENCES)
+            nc.vector.tensor_reduce(out=peak[:, width - 1, :], in_=own, axis=AXIS.X, op=ALU.max)
 
         last_tap = len(chunks) // PARTS - 1
         for step in range(len(chunks) + 2):
@@ -222,51 +232,56 @@ def tile_bertheading_pa_k_kernel(tc, words_emb, W1, b1, W2, b2, W3, b3, out_0, o
                 width, w, tap, part = chunks[closed]
                 if tap == 0:
                     conv[width] = sum_pool.tile([P, TOKENS], F32, name="conv")
-                add_tap(closed // PARTS, 0, TOKENS)
+                add_tap(closed // PARTS, 0, own_tokens(width))
                 if tap == width - 1:
-                    raise_code(width, 0, SENTENCES)
+                    raise_code(width, 0, own_tokens(width))
                     take_peak(width)
 
-        pieces = range(SENTENCES // PIECE)
+        pieces = [slice(i * P, (i + 1) * P) for i in range(TOKEN_TILES)]
         conv[1] = sum_pool.tile([P, TOKENS], F32, name="conv")
-        squares = keep.tile([P, TOKENS], F32)
-        inv_norm = keep.tile([P, TOKENS], F32)
-        words = keep.tile([P, TOKENS], F32)
-        norm_bank = {}
-        for i in pieces:
-            add_tap(last_tap, i * PIECE_TOKENS, (i + 1) * PIECE_TOKENS)
-        for i in pieces:
-            raise_code(1, i * PIECE, (i + 1) * PIECE)
-        for i in pieces:
-            toks = slice(i * PIECE_TOKENS, (i + 1) * PIECE_TOKENS)
-            nc.scalar.activation(out=squares[:, toks], in_=code[:, toks], func=ACT.Square)
-        for i in pieces:
-            toks = slice(i * PIECE_TOKENS, (i + 1) * PIECE_TOKENS)
-            norm_bank[i] = bank_pool.tile([P, PIECE_TOKENS], F32, name="norm_bank", tag="bank")
-            nc.tensor.matmul(out=norm_bank[i][:], lhsT=ones[:], rhs=squares[:, toks], start=True, stop=True)
-
+        code_t = keep.tile([P, TOKENS], F32, align_bytes=64)
+        squares_t = keep.tile([P, TOKENS], F32)
+        part_norm = keep.tile([P, POSITIONS], F32)
+        for i in range(TOKEN_TILES):
+            add_tap(last_tap, i * P, (i + 1) * P)
+        for i in range(TOKEN_TILES + 1):
+            if i < TOKEN_TILES:
+                raise_code(1, i * P, (i + 1) * P)
+            if i >= 1:
+                nc.vector.transpose(out=code_t[:, pieces[i - 1]], in_=code[:, pieces[i - 1]])
+        for cols in pieces:
+            nc.scalar.activation(out=squares_t[:, cols], in_=code_t[:, cols], func=ACT.Square)
+        for i, cols in enumerate(pieces):
+            nc.vector.tensor_reduce(
+                out=part_norm[:, i * TILE_POSITIONS : (i + 1) * TILE_POSITIONS],
+                in_=squares_t[:, cols].rearrange("q (p c) -> q p c", c=BLOCK),
+                axis=AXIS.X,
+                op=ALU.add,
+            )
+        norm_bank = bank_pool.tile([P, POSITIONS], F32, tag="bank")
+        nc.tensor.matmul(out=norm_bank[:], lhsT=fold[:], rhs=part_norm[:], start=True, stop=True)
         take_peak(1)
-        nc.vector.tensor_scalar_max(out=peak[:], in0=peak[:], scalar1=0.0)
-        nc.vector.tensor_reduce(
-            out=pooled_cn[:, 0:SENTENCES], in_=peak[:].rearrange("c k n -> c n k"), axis=AXIS.X, op=ALU.add
+        inv_norm = keep.tile([P, POSITIONS], F32)
+        nc.scalar.activation(out=inv_norm[:], in_=norm_bank[:], func=ACT.Abs_reciprocal_sqrt)
+        words = keep.tile([P, BLOCK, POSITIONS], F32)
+        nc.vector.scalar_tensor_tensor(
+            out=words[:],
+            in0=inv_norm[:].unsqueeze(1).to_broadcast([P, BLOCK, POSITIONS]),
+            scalar=1.0e12,
+            in1=code_t[:].rearrange("q (p c) -> q c p", c=BLOCK),
+            op0=ALU.min,
+            op1=ALU.mult,
         )
+        for b in range(P // BLOCK):
+            nc.sync.dma_start(
+                out=out_0[:, b * BLOCK : (b + 1) * BLOCK, :].rearrange("n c p -> n (c p)"),
+                in_=words[b * BLOCK : (b + 1) * BLOCK].rearrange("q c p -> q (c p)"),
+            )
 
-        for i in pieces:
-            toks = slice(i * PIECE_TOKENS, (i + 1) * PIECE_TOKENS)
-            nc.scalar.activation(out=inv_norm[:, toks], in_=norm_bank[i][:], func=ACT.Abs_reciprocal_sqrt)
-        with nc.allow_non_contiguous_dma(reason="a feature's 20 positions of one sentence are an 80-byte run"):
-            for i in pieces:
-                toks = slice(i * PIECE_TOKENS, (i + 1) * PIECE_TOKENS)
-                nc.vector.scalar_tensor_tensor(
-                    out=words[:, toks], in0=inv_norm[:, toks], scalar=1.0e12, in1=code[:, toks], op0=ALU.min, op1=ALU.mult
-                )
-                nc.sync.dma_start(
-                    out=out_0[i * PIECE : (i + 1) * PIECE].rearrange("n c p -> c n p"),
-                    in_=words[:, toks].rearrange("c (n p) -> c n p", p=POSITIONS),
-                )
-
-        pooled_bank = bank_pool.tile([P, P], F32, tag="bank")
-        nc.tensor.transpose(pooled_bank[:], pooled_cn[:], ident[:])
-        pooled_nc = keep.tile([P, FEATURES], F32)
-        nc.scalar.activation(out=pooled_nc[:], in_=pooled_bank[:], func=ACT.Copy, scale=1.0 / 3.0)
-        nc.scalar.dma_start(out=out_1, in_=pooled_nc[0:SENTENCES, :])
+        nc.vector.tensor_scalar(out=peak[:], in0=peak[:], scalar1=0.0, scalar2=1.0 / 3.0, op0=ALU.max, op1=ALU.mult)
+        pooled_cn = keep.tile([P, SENTENCES], F32, align_bytes=64)
+        nc.vector.tensor_reduce(out=pooled_cn[:], in_=peak[:].rearrange("c k n -> c n k"), axis=AXIS.X, op=ALU.add)
+        pooled_t = keep.tile([P, BLOCK], F32, align_bytes=64)
+        nc.vector.transpose(out=pooled_t[:], in_=pooled_cn[:])
+        for b in range(P // BLOCK):
+            nc.sync.dma_start(out=out_1[:, b * BLOCK : (b + 1) * BLOCK], in_=pooled_t[b * BLOCK : (b + 1) * BLOCK, :])

@@ -24,13 +24,11 @@ MAIN = 512
 REST = TOKENS - MAIN
 
 TILE_POSITIONS = P // SENTENCES
-X_PASSES = 8
-X_PIECE = X_PASSES * K_PASS
-BANK_PASSES = 2
 CHUNK_PASSES = 4
 CHUNK = CHUNK_PASSES * K_PASS
 PARTS = PASSES // CHUNK_PASSES
-W_AHEAD = 6
+BANK_PASSES = 2
+W_AHEAD = 8
 TAP_LAG = 2
 BLOCK = 32
 
@@ -43,8 +41,8 @@ def tile_bertheading_pa_k_kernel(tc, words_emb, W1, b1, W2, b2, W3, b3, out_0, o
     with ExitStack() as stack:
         stack.enter_context(tc.manual_schedule())
         keep = stack.enter_context(tc.tile_pool(name="keep", bufs=1))
-        x_pool = stack.enter_context(tc.tile_pool(name="x_pool", bufs=TOKEN_TILES * PASSES // X_PASSES))
-        xg_pool = stack.enter_context(tc.tile_pool(name="xg_pool", bufs=3))
+        x_pool = stack.enter_context(tc.tile_pool(name="x_pool", bufs=TOKEN_TILES * PARTS))
+        xg_pool = stack.enter_context(tc.tile_pool(name="xg_pool", bufs=4))
         w_pool = stack.enter_context(tc.tile_pool(name="w_pool", bufs=W_AHEAD))
         wg_pool = stack.enter_context(tc.tile_pool(name="wg_pool", bufs=3))
         wq_pool = stack.enter_context(tc.tile_pool(name="wq_pool", bufs=4))
@@ -79,23 +77,22 @@ def tile_bertheading_pa_k_kernel(tc, words_emb, W1, b1, W2, b2, W3, b3, out_0, o
             in_=fold_column[:].unsqueeze(1).to_broadcast([P, P // BLOCK, BLOCK]),
         )
 
-        x_pieces = [(half, tt) for half in range(PASSES // X_PASSES) for tt in range(TOKEN_TILES)]
-        x_raw = {}
-        for i, (half, tt) in enumerate(x_pieces):
-            x_raw[i] = x_pool.tile([P, X_PIECE], BF16, name="x_raw")
-            for a in range(TILE_POSITIONS):
-                nc.sync.dma_start(
-                    out=x_raw[i][a:P:TILE_POSITIONS, :],
-                    in_=words_emb[:, tt * TILE_POSITIONS + a, half * X_PIECE : (half + 1) * X_PIECE],
-                )
-
         chunks = [
             (width, w, tap, part)
             for width, w in ((3, W3), (2, W2), (1, W1))
             for tap in range(width)
             for part in range(PARTS)
         ]
-        w_raw, w_grouped, w_codes, w_scales = {}, {}, {}, {}
+        x_pieces = [(part, tt) for part in range(PARTS) for tt in range(TOKEN_TILES)]
+        x_raw, w_raw, w_grouped, w_codes, w_scales = {}, {}, {}, {}, {}
+
+        def load_x(i):
+            part, tt = x_pieces[i]
+            x_raw[i] = x_pool.tile([P, CHUNK], BF16, name="x_raw")
+            nc.sync.dma_start(
+                out=x_raw[i][:],
+                in_=words_emb[:, tt * TILE_POSITIONS : (tt + 1) * TILE_POSITIONS, part * CHUNK : (part + 1) * CHUNK],
+            )
 
         def load(i):
             width, w, tap, part = chunks[i]
@@ -103,7 +100,11 @@ def tile_bertheading_pa_k_kernel(tc, words_emb, W1, b1, W2, b2, W3, b3, out_0, o
             rows = w[tap, part * CHUNK : (part + 1) * CHUNK, :]
             nc.sync.dma_start(out=w_raw[i][:], in_=rows.rearrange("(g p t) c -> p g t c", p=P, t=PACK))
 
-        for i in range(W_AHEAD):
+        for part in range(PARTS):
+            for tt in range(TOKEN_TILES):
+                load_x(part * TOKEN_TILES + tt)
+            load(part)
+        for i in range(PARTS, W_AHEAD):
             load(i)
 
         x_codes = keep.tile([P, PASSES, TOKENS], U32, align_bytes=64)
@@ -112,58 +113,46 @@ def tile_bertheading_pa_k_kernel(tc, words_emb, W1, b1, W2, b2, W3, b3, out_0, o
 
         def transpose_x(i):
             x_words = x_raw[i][:].bitcast(F32).rearrange("r (g p u) -> r g u p", p=P, u=2)
-            x_grouped[i] = xg_pool.tile([P, X_PASSES * P * PACK], BF16, name="x_grouped", align_bytes=64)
+            x_grouped[i] = xg_pool.tile([P, CHUNK_PASSES * P * PACK], BF16, name="x_grouped", align_bytes=64)
             grouped_words = x_grouped[i][:].bitcast(F32).rearrange("p (g r u) -> p g r u", r=P, u=2)
-            for j in range(X_PASSES // BANK_PASSES):
+            for j in range(CHUNK_PASSES // BANK_PASSES):
                 first = j * BANK_PASSES
                 bank = bank_pool.tile([P, BANK_PASSES, 2, P], F32, tag="bank")
                 for g in range(BANK_PASSES):
                     for u in range(2):
                         nc.tensor.transpose(bank[:, g, u, :], x_words[:, first + g, u, :], perm[:])
-                copy_out = nc.vector.tensor_copy if j % 4 == 3 else nc.scalar.copy
+                bank_no = i * (CHUNK_PASSES // BANK_PASSES) + j
+                copy_out = nc.vector.tensor_copy if bank_no % 4 == 3 else nc.scalar.copy
                 copy_out(
                     out=grouped_words[:, first : first + BANK_PASSES, :, :],
                     in_=bank[:].rearrange("p g u r -> p g r u"),
                 )
 
         def quantise_x(i):
-            half, tt = x_pieces[i]
-            for g in range(X_PASSES):
+            part, tt = x_pieces[i]
+            for g in range(CHUNK_PASSES):
                 nc.vector.quantize_mx(
-                    out=x_codes[:, half * X_PASSES + g, tt * P : (tt + 1) * P].bitcast(FP8X4),
-                    scales=x_scales[:, half * X_PASSES + g, tt * P : (tt + 1) * P],
+                    out=x_codes[:, part * CHUNK_PASSES + g, tt * P : (tt + 1) * P].bitcast(FP8X4),
+                    scales=x_scales[:, part * CHUNK_PASSES + g, tt * P : (tt + 1) * P],
                     in_=x_grouped[i][:, g * P * PACK : (g + 1) * P * PACK],
                 )
 
-        for step in range(len(x_pieces) + 1):
-            if step < len(x_pieces):
-                transpose_x(step)
-            if step >= 1:
-                quantise_x(step - 1)
-
-        bias_rows_f32 = keep.tile([P, P], F32)
-        nc.vector.tensor_copy(out=bias_rows_f32[:], in_=bias_rows[:])
-        bias_bank = bank_pool.tile([P, P], F32, tag="bank")
-        nc.tensor.transpose(bias_bank[:], bias_rows_f32[:], ident[:])
-        bias = keep.tile([P, 3], F32)
-        nc.vector.tensor_copy(out=bias[:], in_=bias_bank[:, 0:3])
-
         acc, conv = {}, {}
+        bias = keep.tile([P, 3], F32)
         peak = keep.tile([P, 3, SENTENCES], F32)
 
         def regroup(i):
             w_grouped[i] = wg_pool.tile([P, CHUNK_PASSES, FEATURES, PACK], BF16, name="w_grouped", align_bytes=64)
-            if i % 2 == 0:
-                nc.vector.tensor_copy(
-                    out=w_grouped[i][:].rearrange("p g (c i) t -> p g c t i", i=4),
-                    in_=w_raw[i][:].rearrange("p g t (c i) -> p g c t i", i=4),
+            half = CHUNK_PASSES // 2
+            nc.vector.tensor_copy(
+                out=w_grouped[i][:, 0:half].rearrange("p g (c i) t -> p g c t i", i=4),
+                in_=w_raw[i][:, 0:half].rearrange("p g t (c i) -> p g c t i", i=4),
+            )
+            for g in range(half, CHUNK_PASSES):
+                nc.scalar.copy(
+                    out=w_grouped[i][:, g].rearrange("p (c i) t -> p c t i", i=4),
+                    in_=w_raw[i][:, g].rearrange("p t (c i) -> p c t i", i=4),
                 )
-            else:
-                for g in range(CHUNK_PASSES):
-                    nc.scalar.copy(
-                        out=w_grouped[i][:, g].rearrange("p (c i) t -> p c t i", i=4),
-                        in_=w_raw[i][:, g].rearrange("p t (c i) -> p c t i", i=4),
-                    )
 
         def quantise(i):
             w_codes[i] = wq_pool.tile([P, CHUNK_PASSES * FEATURES], U32, name="w_codes", align_bytes=64)
@@ -211,14 +200,17 @@ def tile_bertheading_pa_k_kernel(tc, words_emb, W1, b1, W2, b2, W3, b3, out_0, o
                         nc.vector.tensor_tensor(out=dst, in0=dst, in1=product, op=ALU.add)
 
         def raise_code(width, lo, hi):
-            nc.vector.tensor_tensor(out=code[:, lo:hi], in0=code[:, lo:hi], in1=conv[width][:, lo:hi], op=ALU.max)
+            nc.vector.scalar_tensor_tensor(
+                out=code[:, lo:hi], in0=conv[width][:, lo:hi], scalar=0.0, in1=code[:, lo:hi], op0=ALU.max, op1=ALU.max
+            )
 
         def take_peak(width):
             own = conv[width][:, 0 : own_tokens(width)].rearrange("c (p n) -> c n p", n=SENTENCES)
             nc.vector.tensor_reduce(out=peak[:, width - 1, :], in_=own, axis=AXIS.X, op=ALU.max)
 
         last_tap = len(chunks) // PARTS - 1
-        for step in range(len(chunks) + 2):
+
+        def pipeline_step(step):
             if step < len(chunks):
                 regroup(step)
             if step + W_AHEAD < len(chunks):
@@ -231,11 +223,31 @@ def tile_bertheading_pa_k_kernel(tc, words_emb, W1, b1, W2, b2, W3, b3, out_0, o
             if closed >= 0 and closed % PARTS == PARTS - 1 and closed // PARTS < last_tap:
                 width, w, tap, part = chunks[closed]
                 if tap == 0:
-                    conv[width] = sum_pool.tile([P, TOKENS], F32, name="conv")
+                    conv[width] = code if width == 3 else sum_pool.tile([P, TOKENS], F32, name="conv")
                 add_tap(closed // PARTS, 0, own_tokens(width))
                 if tap == width - 1:
-                    raise_code(width, 0, own_tokens(width))
                     take_peak(width)
+                    if width < 3:
+                        raise_code(width, 0, own_tokens(width))
+
+        for part in range(PARTS):
+            for tt in range(TOKEN_TILES):
+                i = part * TOKEN_TILES + tt
+                transpose_x(i)
+                if i >= 1:
+                    quantise_x(i - 1)
+            if part == PARTS - 1:
+                quantise_x(len(x_pieces) - 1)
+            pipeline_step(part)
+
+        bias_rows_f32 = keep.tile([P, P], F32)
+        nc.vector.tensor_copy(out=bias_rows_f32[:], in_=bias_rows[:])
+        bias_bank = bank_pool.tile([P, P], F32, tag="bank")
+        nc.tensor.transpose(bias_bank[:], bias_rows_f32[:], ident[:])
+        nc.vector.tensor_copy(out=bias[:], in_=bias_bank[:, 0:3])
+
+        for step in range(PARTS, len(chunks) + 2):
+            pipeline_step(step)
 
         pieces = [slice(i * P, (i + 1) * P) for i in range(TOKEN_TILES)]
         conv[1] = sum_pool.tile([P, TOKENS], F32, name="conv")

@@ -6,6 +6,7 @@ from concourse.masks import make_identity
 F32 = mybir.dt.float32
 BF16 = mybir.dt.bfloat16
 U32 = mybir.dt.uint32
+I32 = mybir.dt.int32
 U8 = mybir.dt.uint8
 FP8X4 = mybir.dt.float8_e4m3fn_x4
 ALU = mybir.AluOpType
@@ -17,19 +18,22 @@ PACK = 4
 K_PASS = P * PACK
 
 SENTENCES, POSITIONS, EMBED, FEATURES = 32, 20, 8192, 128
+WIDTHS = (3, 2, 1)
 TOKENS = SENTENCES * POSITIONS
 PASSES = EMBED // K_PASS
 TOKEN_TILES = TOKENS // P
 MAIN = 512
 REST = TOKENS - MAIN
+PAD = (max(WIDTHS) - 1) * SENTENCES
 
 TILE_POSITIONS = P // SENTENCES
-CHUNK_PASSES = 4
-CHUNK = CHUNK_PASSES * K_PASS
-PARTS = PASSES // CHUNK_PASSES
+PART_PASSES = 4
+PART = PART_PASSES * K_PASS
+PARTS = PASSES // PART_PASSES
 BANK_PASSES = 2
-W_AHEAD = 8
-TAP_LAG = 2
+X_GROUP, W_GROUP = 2, 2
+W_START = 2
+LOADS_AHEAD = 12
 BLOCK = 32
 
 FLOPS = 2 * EMBED * FEATURES * SENTENCES * (20 * 1 + 19 * 2 + 18 * 3)
@@ -41,14 +45,13 @@ def tile_bertheading_pa_k_kernel(tc, words_emb, W1, b1, W2, b2, W3, b3, out_0, o
     with ExitStack() as stack:
         stack.enter_context(tc.manual_schedule())
         keep = stack.enter_context(tc.tile_pool(name="keep", bufs=1))
-        x_pool = stack.enter_context(tc.tile_pool(name="x_pool", bufs=TOKEN_TILES * PARTS))
-        xg_pool = stack.enter_context(tc.tile_pool(name="xg_pool", bufs=4))
-        w_pool = stack.enter_context(tc.tile_pool(name="w_pool", bufs=W_AHEAD))
-        wg_pool = stack.enter_context(tc.tile_pool(name="wg_pool", bufs=3))
-        wq_pool = stack.enter_context(tc.tile_pool(name="wq_pool", bufs=4))
-        sum_pool = stack.enter_context(tc.tile_pool(name="sum_pool", bufs=2))
+        x_pool = stack.enter_context(tc.tile_pool(name="x_pool", bufs=8))
+        xg_pool = stack.enter_context(tc.tile_pool(name="xg_pool", bufs=2))
+        w_pool = stack.enter_context(tc.tile_pool(name="w_pool", bufs=12))
+        wg_pool = stack.enter_context(tc.tile_pool(name="wg_pool", bufs=4))
+        wq_pool = stack.enter_context(tc.tile_pool(name="wq_pool", bufs=6))
         bank_pool = stack.enter_context(tc.psum_pool(name="bank_pool", bufs=4))
-        acc_pool = stack.enter_context(tc.psum_pool(name="acc_pool", bufs=2))
+        acc_pool = stack.enter_context(tc.psum_pool(name="acc_pool", bufs=1))
 
         warm = keep.tile([P, 1], F32)
         nc.vector.memset(warm[:], 1.0)
@@ -56,11 +59,9 @@ def tile_bertheading_pa_k_kernel(tc, words_emb, W1, b1, W2, b2, W3, b3, out_0, o
 
         ident = keep.tile([P, P], F32)
         make_identity(nc, ident[:])
-        code = keep.tile([P, TOKENS], F32, align_bytes=64)
-        nc.vector.memset(code[:], 0.0)
         bias_rows = keep.tile([P, P], BF16)
         nc.vector.memset(bias_rows[:], 0.0)
-        for row, b in enumerate((b1, b2, b3)):
+        for row, b in enumerate((b3, b2, b1)):
             nc.scalar.dma_start(out=bias_rows[row : row + 1, :], in_=b.unsqueeze(0))
 
         perm = keep.tile([P, P], F32)
@@ -77,127 +78,163 @@ def tile_bertheading_pa_k_kernel(tc, words_emb, W1, b1, W2, b2, W3, b3, out_0, o
             in_=fold_column[:].unsqueeze(1).to_broadcast([P, P // BLOCK, BLOCK]),
         )
 
-        chunks = [
-            (width, w, tap, part)
-            for width, w in ((3, W3), (2, W2), (1, W1))
-            for tap in range(width)
-            for part in range(PARTS)
-        ]
-        x_pieces = [(part, tt) for part in range(PARTS) for tt in range(TOKEN_TILES)]
-        x_raw, w_raw, w_grouped, w_codes, w_scales = {}, {}, {}, {}, {}
+        x_codes = keep.tile([P, PASSES, TOKENS + PAD], U32, align_bytes=64)
+        x_scales = keep.tile([P, PASSES, TOKENS + PAD], U8, align_bytes=64)
+        x_scales_moved = keep.tile([P, PASSES, TOKENS], U8, align_bytes=64)
+        nc.vector.memset(x_codes[:, :, TOKENS:], 0)
+        nc.vector.memset(x_scales[:].bitcast(I32), 0)
+        code = keep.tile([P, TOKENS], F32, align_bytes=64)
+        nc.vector.memset(code[:], 0.0)
 
-        def load_x(i):
-            part, tt = x_pieces[i]
-            x_raw[i] = x_pool.tile([P, CHUNK], BF16, name="x_raw")
-            nc.sync.dma_start(
-                out=x_raw[i][:],
-                in_=words_emb[:, tt * TILE_POSITIONS : (tt + 1) * TILE_POSITIONS, part * CHUNK : (part + 1) * CHUNK],
-            )
+        taps = [(width, tap) for width in WIDTHS for tap in range(width)]
+        weights = {3: W3, 2: W2, 1: W1}
+        x_items = [("x", part, tt) for part in range(PARTS) for tt in range(TOKEN_TILES)]
+        w_items = [("w", part, i) for part in range(PARTS) for i in range(len(taps))]
+        x_steps = [x_items[i : i + X_GROUP] for i in range(0, len(x_items), X_GROUP)]
+        paired = W_GROUP * (len(x_steps) - W_START)
+        w_steps = [[]] * W_START + [w_items[i : i + W_GROUP] for i in range(0, paired, W_GROUP)] + [[item] for item in w_items[paired:]]
+        steps = len(w_steps)
+        x_steps += [[]] * (steps - len(x_steps))
+        load_order = [item for step in range(steps) for item in x_steps[step] + w_steps[step]]
+        raw, grouped, x_grouped, banks, w_codes, w_scales = {}, {}, {}, {}, {}, {}
 
-        def load(i):
-            width, w, tap, part = chunks[i]
-            w_raw[i] = w_pool.tile([P, CHUNK_PASSES, PACK, FEATURES], BF16, name="w_raw")
-            rows = w[tap, part * CHUNK : (part + 1) * CHUNK, :]
-            nc.sync.dma_start(out=w_raw[i][:], in_=rows.rearrange("(g p t) c -> p g t c", p=P, t=PACK))
+        def load(item):
+            kind, part, i = item
+            if kind == "x":
+                raw[item] = x_pool.tile([P, PART], BF16, name="x_raw")
+                src = words_emb[:, i * TILE_POSITIONS : (i + 1) * TILE_POSITIONS, part * PART : (part + 1) * PART]
+            else:
+                width, tap = taps[i]
+                raw[item] = w_pool.tile([P, PART_PASSES, PACK, FEATURES], BF16, name="w_raw")
+                rows = weights[width][tap, part * PART : (part + 1) * PART, :]
+                src = rows.rearrange("(g p t) c -> p g t c", p=P, t=PACK)
+            nc.sync.dma_start(out=raw[item][:], in_=src)
 
-        for part in range(PARTS):
-            for tt in range(TOKEN_TILES):
-                load_x(part * TOKEN_TILES + tt)
-            load(part)
-        for i in range(PARTS, W_AHEAD):
-            load(i)
+        for item in load_order[:LOADS_AHEAD]:
+            load(item)
 
-        x_codes = keep.tile([P, PASSES, TOKENS], U32, align_bytes=64)
-        x_scales = keep.tile([P, PASSES, TOKENS], U8, align_bytes=64)
-        x_grouped = {}
+        bias = keep.tile([P, len(WIDTHS)], F32)
+        peak = keep.tile([P, len(WIDTHS), SENTENCES], F32)
+        main = [acc_pool.tile([P, MAIN], F32, name=f"main_{width}") for width in WIDTHS]
+        rest_sum = keep.tile([P, len(WIDTHS), REST], F32)
+        rest = {}
+        conv = {}
 
-        def transpose_x(i):
-            x_words = x_raw[i][:].bitcast(F32).rearrange("r (g p u) -> r g u p", p=P, u=2)
-            x_grouped[i] = xg_pool.tile([P, CHUNK_PASSES * P * PACK], BF16, name="x_grouped", align_bytes=64)
-            grouped_words = x_grouped[i][:].bitcast(F32).rearrange("p (g r u) -> p g r u", r=P, u=2)
-            for j in range(CHUNK_PASSES // BANK_PASSES):
+        def transpose_x(item):
+            part, tt = item[1:]
+            if tt == 0:
+                x_grouped[part] = xg_pool.tile([P, PART_PASSES, TOKENS, PACK], BF16, name="x_grouped", align_bytes=64)
+            x_words = raw[item][:].bitcast(F32).rearrange("r (g p u) -> r g u p", p=P, u=2)
+            for j in range(PART_PASSES // BANK_PASSES):
                 first = j * BANK_PASSES
                 bank = bank_pool.tile([P, BANK_PASSES, 2, P], F32, tag="bank")
+                banks[item, j] = bank
                 for g in range(BANK_PASSES):
                     for u in range(2):
                         nc.tensor.transpose(bank[:, g, u, :], x_words[:, first + g, u, :], perm[:])
-                bank_no = i * (CHUNK_PASSES // BANK_PASSES) + j
-                copy_out = nc.vector.tensor_copy if bank_no % 4 == 3 else nc.scalar.copy
-                copy_out(
-                    out=grouped_words[:, first : first + BANK_PASSES, :, :],
-                    in_=bank[:].rearrange("p g u r -> p g r u"),
-                )
 
-        def quantise_x(i):
-            part, tt = x_pieces[i]
-            for g in range(CHUNK_PASSES):
-                nc.vector.quantize_mx(
-                    out=x_codes[:, part * CHUNK_PASSES + g, tt * P : (tt + 1) * P].bitcast(FP8X4),
-                    scales=x_scales[:, part * CHUNK_PASSES + g, tt * P : (tt + 1) * P],
-                    in_=x_grouped[i][:, g * P * PACK : (g + 1) * P * PACK],
-                )
-
-        acc, conv = {}, {}
-        bias = keep.tile([P, 3], F32)
-        peak = keep.tile([P, 3, SENTENCES], F32)
-
-        def regroup(i):
-            w_grouped[i] = wg_pool.tile([P, CHUNK_PASSES, FEATURES, PACK], BF16, name="w_grouped", align_bytes=64)
-            half = CHUNK_PASSES // 2
-            nc.vector.tensor_copy(
-                out=w_grouped[i][:, 0:half].rearrange("p g (c i) t -> p g c t i", i=4),
-                in_=w_raw[i][:, 0:half].rearrange("p g t (c i) -> p g c t i", i=4),
-            )
-            for g in range(half, CHUNK_PASSES):
+        def copy_x(item):
+            part, tt = item[1:]
+            grouped_words = x_grouped[part][:].rearrange("p g r t -> p (g r t)").bitcast(F32)
+            grouped_words = grouped_words.rearrange("p (g r u) -> p g r u", g=PART_PASSES, u=2)
+            for j in range(PART_PASSES // BANK_PASSES):
+                first = j * BANK_PASSES
                 nc.scalar.copy(
-                    out=w_grouped[i][:, g].rearrange("p (c i) t -> p c t i", i=4),
-                    in_=w_raw[i][:, g].rearrange("p t (c i) -> p c t i", i=4),
+                    out=grouped_words[:, first : first + BANK_PASSES, tt * P : (tt + 1) * P, :],
+                    in_=banks[item, j][:].rearrange("p g u r -> p g r u"),
                 )
 
-        def quantise(i):
-            w_codes[i] = wq_pool.tile([P, CHUNK_PASSES * FEATURES], U32, name="w_codes", align_bytes=64)
-            w_scales[i] = wq_pool.tile([P, CHUNK_PASSES * FEATURES], U8, name="w_scales", align_bytes=64)
-            nc.vector.quantize_mx(
-                out=w_codes[i][:].bitcast(FP8X4),
-                scales=w_scales[i][:],
-                in_=w_grouped[i][:].rearrange("p g c t -> p (g c t)"),
+        def quantise_x(part, first, last):
+            for g in range(PART_PASSES):
+                k_pass = part * PART_PASSES + g
+                nc.vector.quantize_mx(
+                    out=x_codes[:, k_pass, first:last].bitcast(FP8X4),
+                    scales=x_scales[:, k_pass, first:last],
+                    in_=x_grouped[part][:, g, first:last, :].rearrange("p r t -> p (r t)"),
+                )
+
+        def move_scales(part):
+            ks = slice(part * PART_PASSES, (part + 1) * PART_PASSES)
+            nc.vector.tensor_copy(
+                out=x_scales_moved[:, ks, :].bitcast(I32), in_=x_scales[:, ks, SENTENCES : SENTENCES + TOKENS].bitcast(I32)
             )
 
-        def multiply(i):
-            part = i % PARTS
-            if part == 0:
-                acc_main = acc_pool.tile([P, MAIN], F32)
-                acc_rest = acc_pool.tile([P, REST], F32)
-                acc[i // PARTS] = (acc_main, acc_rest)
-            for g in range(CHUNK_PASSES):
-                k_pass = part * CHUNK_PASSES + g
+        def regroup(item):
+            grouped[item] = wg_pool.tile([P, PART_PASSES, FEATURES, PACK], BF16, name="w_grouped", align_bytes=64)
+            half = PART_PASSES // 2
+            nc.vector.tensor_copy(
+                out=grouped[item][:, 0:half].rearrange("p g (c i) t -> p g c t i", i=4),
+                in_=raw[item][:, 0:half].rearrange("p g t (c i) -> p g c t i", i=4),
+            )
+            for g in range(half, PART_PASSES):
+                nc.scalar.copy(
+                    out=grouped[item][:, g].rearrange("p (c i) t -> p c t i", i=4),
+                    in_=raw[item][:, g].rearrange("p t (c i) -> p c t i", i=4),
+                )
+
+        def quantise_w(item):
+            w_codes[item] = wq_pool.tile([P, PART_PASSES * FEATURES], U32, name="w_codes", align_bytes=64)
+            w_scales[item] = wq_pool.tile([P, PART_PASSES * FEATURES], U8, name="w_scales", align_bytes=64)
+            nc.vector.quantize_mx(
+                out=w_codes[item][:].bitcast(FP8X4),
+                scales=w_scales[item][:],
+                in_=grouped[item][:].rearrange("p g c t -> p (g c t)"),
+            )
+
+        def multiply(item):
+            part, i = item[1:]
+            width, tap = taps[i]
+            s = WIDTHS.index(width)
+            if part < PARTS - 1:
+                if i == 0:
+                    rest[part] = acc_pool.tile([P, len(WIDTHS), REST], F32, name="rest")
+                rest_out = rest[part][:, s, :]
+            else:
+                if tap == 0:
+                    rest[part, s] = bank_pool.tile([P, REST], F32, tag="bank", name="rest_last")
+                rest_out = rest[part, s][:]
+            shift = tap * SENTENCES
+            for g in range(PART_PASSES):
+                k_pass = part * PART_PASSES + g
                 cols = slice(g * FEATURES, (g + 1) * FEATURES)
-                for bank, toks in zip(acc[i // PARTS], (slice(0, MAIN), slice(MAIN, TOKENS))):
+                opens, closes = tap == 0 and g == 0, tap == width - 1 and g == PART_PASSES - 1
+                for out, tokens, start, stop in (
+                    (main[s][:], slice(shift, shift + MAIN), opens and part == 0, closes and part == PARTS - 1),
+                    (rest_out, slice(shift + MAIN, shift + TOKENS), opens, closes),
+                ):
+                    scales = x_scales[:, k_pass, tokens]
+                    if tap == 1:
+                        scales = x_scales_moved[:, k_pass, tokens.start - shift : tokens.stop - shift]
                     nc.tensor.matmul_mx(
-                        out=bank[:],
-                        lhsT=w_codes[i][:, cols].bitcast(FP8X4),
-                        lhsT_scale=w_scales[i][:, cols],
-                        rhs=x_codes[:, k_pass, toks].bitcast(FP8X4),
-                        rhs_scale=x_scales[:, k_pass, toks],
-                        start=(k_pass == 0),
-                        stop=(k_pass == PASSES - 1),
+                        out=out,
+                        lhsT=w_codes[item][:, cols].bitcast(FP8X4),
+                        lhsT_scale=w_scales[item][:, cols],
+                        rhs=x_codes[:, k_pass, tokens].bitcast(FP8X4),
+                        rhs_scale=scales,
+                        start=start,
+                        stop=stop,
                     )
+
+        def add_rest(part):
+            base = bias[:].unsqueeze(2).to_broadcast([P, len(WIDTHS), REST]) if part == 0 else rest_sum[:]
+            nc.vector.tensor_tensor(out=rest_sum[:], in0=rest[part][:], in1=base, op=ALU.add)
 
         def own_tokens(width):
             return (POSITIONS - width + 1) * SENTENCES
 
-        def add_tap(tap_no, lo, hi):
-            width, w, tap, part = chunks[tap_no * PARTS]
-            shift = tap * SENTENCES
-            cut = min(max(MAIN - shift, lo), hi)
-            for bank, dst_lo, dst_hi, src_lo in ((0, lo, cut, lo + shift), (1, cut, hi, cut + shift - MAIN)):
-                if dst_lo < dst_hi:
-                    dst = conv[width][:, dst_lo:dst_hi]
-                    product = acc[tap_no][bank][:, src_lo : src_lo + dst_hi - dst_lo]
-                    if tap == 0:
-                        nc.scalar.activation(out=dst, in_=product, func=ACT.Identity, bias=bias[:, width - 1 : width])
-                    else:
-                        nc.vector.tensor_tensor(out=dst, in0=dst, in1=product, op=ALU.add)
+        def finish_main(width, lo, hi):
+            s = WIDTHS.index(width)
+            nc.scalar.activation(out=conv[width][:, lo:hi], in_=main[s][:, lo:hi], func=ACT.Identity, bias=bias[:, s : s + 1])
+
+        def finish_rest(width):
+            s = WIDTHS.index(width)
+            hi = own_tokens(width)
+            nc.vector.tensor_tensor(
+                out=conv[width][:, MAIN:hi],
+                in0=rest[PARTS - 1, s][:, 0 : hi - MAIN],
+                in1=rest_sum[:, s, 0 : hi - MAIN],
+                op=ALU.add,
+            )
 
         def raise_code(width, lo, hi):
             nc.vector.scalar_tensor_tensor(
@@ -206,56 +243,70 @@ def tile_bertheading_pa_k_kernel(tc, words_emb, W1, b1, W2, b2, W3, b3, out_0, o
 
         def take_peak(width):
             own = conv[width][:, 0 : own_tokens(width)].rearrange("c (p n) -> c n p", n=SENTENCES)
-            nc.vector.tensor_reduce(out=peak[:, width - 1, :], in_=own, axis=AXIS.X, op=ALU.max)
+            nc.vector.tensor_reduce(out=peak[:, WIDTHS.index(width), :], in_=own, axis=AXIS.X, op=ALU.max)
 
-        last_tap = len(chunks) // PARTS - 1
+        def after_multiply(item):
+            part, i = item[1:]
+            width, tap = taps[i]
+            if part < PARTS - 1:
+                if i == len(taps) - 1:
+                    add_rest(part)
+            elif width > 1 and tap == width - 1:
+                conv[width] = code if width == 3 else keep.tile([P, TOKENS], F32, name="conv_2")
+                finish_main(width, 0, MAIN)
+                finish_rest(width)
+                if width == 2:
+                    raise_code(width, 0, own_tokens(width))
+                take_peak(width)
 
-        def pipeline_step(step):
-            if step < len(chunks):
-                regroup(step)
-            if step + W_AHEAD < len(chunks):
-                load(step + W_AHEAD)
-            if 1 <= step <= len(chunks):
-                quantise(step - 1)
-            if step >= 2:
-                multiply(step - 2)
-            closed = step - 2 - TAP_LAG
-            if closed >= 0 and closed % PARTS == PARTS - 1 and closed // PARTS < last_tap:
-                width, w, tap, part = chunks[closed]
-                if tap == 0:
-                    conv[width] = code if width == 3 else sum_pool.tile([P, TOKENS], F32, name="conv")
-                add_tap(closed // PARTS, 0, own_tokens(width))
-                if tap == width - 1:
-                    take_peak(width)
-                    if width < 3:
-                        raise_code(width, 0, own_tokens(width))
-
-        for part in range(PARTS):
-            for tt in range(TOKEN_TILES):
-                i = part * TOKEN_TILES + tt
-                transpose_x(i)
-                if i >= 1:
-                    quantise_x(i - 1)
-            if part == PARTS - 1:
-                quantise_x(len(x_pieces) - 1)
-            pipeline_step(part)
-
-        bias_rows_f32 = keep.tile([P, P], F32)
-        nc.vector.tensor_copy(out=bias_rows_f32[:], in_=bias_rows[:])
-        bias_bank = bank_pool.tile([P, P], F32, tag="bank")
-        nc.tensor.transpose(bias_bank[:], bias_rows_f32[:], ident[:])
-        nc.vector.tensor_copy(out=bias[:], in_=bias_bank[:, 0:3])
-
-        for step in range(PARTS, len(chunks) + 2):
-            pipeline_step(step)
+        loaded = LOADS_AHEAD
+        for step in range(steps + 2):
+            now_x, now_w = (x_steps[step], w_steps[step]) if step < steps else ([], [])
+            last_x, last_w = (x_steps[step - 1], w_steps[step - 1]) if 1 <= step <= steps else ([], [])
+            ready_w = w_steps[step - 2] if step >= 2 else []
+            done_w = w_steps[step - 3] if step >= 3 else []
+            for item in now_x:
+                transpose_x(item)
+            for item in done_w:
+                if item[1] < PARTS - 1:
+                    after_multiply(item)
+            for item in now_w[:1]:
+                regroup(item)
+            for item in now_x:
+                copy_x(item)
+            for item in now_w[1:]:
+                regroup(item)
+            for item in load_order[loaded : loaded + len(now_x) + len(now_w)]:
+                load(item)
+            loaded += len(now_x) + len(now_w)
+            for part in sorted({item[1] for item in last_x}):
+                tiles = [item[2] for item in last_x if item[1] == part]
+                quantise_x(part, tiles[0] * P, (tiles[-1] + 1) * P)
+            for item in last_w:
+                quantise_w(item)
+            for item in last_x:
+                if item[2] == TOKEN_TILES - 1:
+                    move_scales(item[1])
+            for item in done_w:
+                if item[1] == PARTS - 1:
+                    after_multiply(item)
+            for item in ready_w:
+                multiply(item)
+            if step == W_START:
+                bias_rows_f32 = keep.tile([P, P], F32)
+                nc.vector.tensor_copy(out=bias_rows_f32[:], in_=bias_rows[:])
+                bias_bank = bank_pool.tile([P, P], F32, tag="bank")
+                nc.tensor.transpose(bias_bank[:], bias_rows_f32[:], ident[:])
+                nc.vector.tensor_copy(out=bias[:], in_=bias_bank[:, 0 : len(WIDTHS)])
 
         pieces = [slice(i * P, (i + 1) * P) for i in range(TOKEN_TILES)]
-        conv[1] = sum_pool.tile([P, TOKENS], F32, name="conv")
+        conv[1] = keep.tile([P, TOKENS], F32, name="conv_1")
         code_t = keep.tile([P, TOKENS], F32, align_bytes=64)
         squares_t = keep.tile([P, TOKENS], F32)
         part_norm = keep.tile([P, POSITIONS], F32)
-        for i in range(TOKEN_TILES):
-            add_tap(last_tap, i * P, (i + 1) * P)
+        for i in range(MAIN // P):
+            finish_main(1, i * P, (i + 1) * P)
+        finish_rest(1)
         for i in range(TOKEN_TILES + 1):
             if i < TOKEN_TILES:
                 raise_code(1, i * P, (i + 1) * P)

@@ -18,7 +18,7 @@ PACK = 4
 K_PASS = P * PACK
 
 SENTENCES, POSITIONS, EMBED, FEATURES = 32, 20, 8192, 128
-WIDTHS = (3, 2, 1)
+WIDTHS = (1, 2, 3)
 TOKENS = SENTENCES * POSITIONS
 PASSES = EMBED // K_PASS
 TOKEN_TILES = TOKENS // P
@@ -28,11 +28,9 @@ PAD = (max(WIDTHS) - 1) * SENTENCES
 
 TILE_POSITIONS = P // SENTENCES
 PART_PASSES = 4
-PART = PART_PASSES * K_PASS
 PARTS = PASSES // PART_PASSES
 BANK_PASSES = 2
-X_GROUP, W_GROUP = 2, 2
-W_START = 2
+MULTIPLY_LAG = 2
 LOADS_AHEAD = 12
 BLOCK = 32
 
@@ -48,7 +46,7 @@ def tile_bertheading_pa_k_kernel(tc, words_emb, W1, b1, W2, b2, W3, b3, out_0, o
         x_pool = stack.enter_context(tc.tile_pool(name="x_pool", bufs=8))
         xg_pool = stack.enter_context(tc.tile_pool(name="xg_pool", bufs=2))
         w_pool = stack.enter_context(tc.tile_pool(name="w_pool", bufs=12))
-        wg_pool = stack.enter_context(tc.tile_pool(name="wg_pool", bufs=4))
+        wg_pool = stack.enter_context(tc.tile_pool(name="wg_pool", bufs=3))
         wq_pool = stack.enter_context(tc.tile_pool(name="wq_pool", bufs=6))
         bank_pool = stack.enter_context(tc.psum_pool(name="bank_pool", bufs=4))
         acc_pool = stack.enter_context(tc.psum_pool(name="acc_pool", bufs=1))
@@ -61,53 +59,45 @@ def tile_bertheading_pa_k_kernel(tc, words_emb, W1, b1, W2, b2, W3, b3, out_0, o
         make_identity(nc, ident[:])
         bias_rows = keep.tile([P, P], BF16)
         nc.vector.memset(bias_rows[:], 0.0)
-        for row, b in enumerate((b3, b2, b1)):
+        for row, b in enumerate((b1, b2, b3)):
             nc.scalar.dma_start(out=bias_rows[row : row + 1, :], in_=b.unsqueeze(0))
 
         perm = keep.tile([P, P], F32)
         nc.vector.tensor_copy(
             out=perm[:].rearrange("i (a n) -> i a n", n=SENTENCES), in_=ident[:].rearrange("i (n a) -> i a n", n=SENTENCES)
         )
-        fold_column = keep.tile([P, BLOCK], F32)
-        nc.vector.tensor_reduce(
-            out=fold_column[:], in_=ident[:].rearrange("i (b n) -> i n b", n=BLOCK), axis=AXIS.X, op=ALU.add
-        )
-        fold = keep.tile([P, P], F32)
-        nc.vector.tensor_copy(
-            out=fold[:].rearrange("i (b n) -> i b n", n=BLOCK),
-            in_=fold_column[:].unsqueeze(1).to_broadcast([P, P // BLOCK, BLOCK]),
-        )
-
         x_codes = keep.tile([P, PASSES, TOKENS + PAD], U32, align_bytes=64)
         x_scales = keep.tile([P, PASSES, TOKENS + PAD], U8, align_bytes=64)
         x_scales_moved = keep.tile([P, PASSES, TOKENS], U8, align_bytes=64)
-        nc.vector.memset(x_codes[:, :, TOKENS:], 0)
-        nc.vector.memset(x_scales[:].bitcast(I32), 0)
+        nc.gpsimd.memset(x_codes[:, :, TOKENS:], 0)
+        nc.gpsimd.memset(x_scales[:].bitcast(I32), 0)
         code = keep.tile([P, TOKENS], F32, align_bytes=64)
-        nc.vector.memset(code[:], 0.0)
+        pooled_cn = keep.tile([P, P], F32)
+        nc.gpsimd.memset(pooled_cn[:], 0.0)
 
         taps = [(width, tap) for width in WIDTHS for tap in range(width)]
         weights = {3: W3, 2: W2, 1: W1}
-        x_items = [("x", part, tt) for part in range(PARTS) for tt in range(TOKEN_TILES)]
-        w_items = [("w", part, i) for part in range(PARTS) for i in range(len(taps))]
-        x_steps = [x_items[i : i + X_GROUP] for i in range(0, len(x_items), X_GROUP)]
-        paired = W_GROUP * (len(x_steps) - W_START)
-        w_steps = [[]] * W_START + [w_items[i : i + W_GROUP] for i in range(0, paired, W_GROUP)] + [[item] for item in w_items[paired:]]
+        x_steps = [[("x", 0, tt)] for tt in range(TOKEN_TILES)]
+        w_steps = [[] for step in x_steps]
+        for part in range(PARTS):
+            for i in range(len(taps)):
+                x_steps.append([("x", part + 1, i)] if i < TOKEN_TILES and part + 1 < PARTS else [])
+                w_steps.append([("w", part, i)])
         steps = len(w_steps)
-        x_steps += [[]] * (steps - len(x_steps))
         load_order = [item for step in range(steps) for item in x_steps[step] + w_steps[step]]
         raw, grouped, x_grouped, banks, w_codes, w_scales = {}, {}, {}, {}, {}, {}
 
         def load(item):
             kind, part, i = item
+            passes = PART_PASSES
+            rows = slice(part * PART_PASSES * K_PASS, (part * PART_PASSES + passes) * K_PASS)
             if kind == "x":
-                raw[item] = x_pool.tile([P, PART], BF16, name="x_raw")
-                src = words_emb[:, i * TILE_POSITIONS : (i + 1) * TILE_POSITIONS, part * PART : (part + 1) * PART]
+                raw[item] = x_pool.tile([P, passes * K_PASS], BF16, name="x_raw")
+                src = words_emb[:, i * TILE_POSITIONS : (i + 1) * TILE_POSITIONS, rows]
             else:
                 width, tap = taps[i]
-                raw[item] = w_pool.tile([P, PART_PASSES, PACK, FEATURES], BF16, name="w_raw")
-                rows = weights[width][tap, part * PART : (part + 1) * PART, :]
-                src = rows.rearrange("(g p t) c -> p g t c", p=P, t=PACK)
+                raw[item] = w_pool.tile([P, passes, PACK, FEATURES], BF16, name="w_raw")
+                src = weights[width][tap, rows, :].rearrange("(g p t) c -> p g t c", p=P, t=PACK)
             nc.sync.dma_start(out=raw[item][:], in_=src)
 
         for item in load_order[:LOADS_AHEAD]:
@@ -136,7 +126,7 @@ def tile_bertheading_pa_k_kernel(tc, words_emb, W1, b1, W2, b2, W3, b3, out_0, o
         def copy_x(item):
             part, tt = item[1:]
             grouped_words = x_grouped[part][:].rearrange("p g r t -> p (g r t)").bitcast(F32)
-            grouped_words = grouped_words.rearrange("p (g r u) -> p g r u", g=PART_PASSES, u=2)
+            grouped_words = grouped_words.rearrange("p (g r u) -> p g r u", r=TOKENS, u=2)
             for j in range(PART_PASSES // BANK_PASSES):
                 first = j * BANK_PASSES
                 nc.scalar.copy(
@@ -154,27 +144,29 @@ def tile_bertheading_pa_k_kernel(tc, words_emb, W1, b1, W2, b2, W3, b3, out_0, o
                 )
 
         def move_scales(part):
-            ks = slice(part * PART_PASSES, (part + 1) * PART_PASSES)
+            ks = slice(part * PART_PASSES, part * PART_PASSES + PART_PASSES)
             nc.vector.tensor_copy(
                 out=x_scales_moved[:, ks, :].bitcast(I32), in_=x_scales[:, ks, SENTENCES : SENTENCES + TOKENS].bitcast(I32)
             )
 
         def regroup(item):
-            grouped[item] = wg_pool.tile([P, PART_PASSES, FEATURES, PACK], BF16, name="w_grouped", align_bytes=64)
-            half = PART_PASSES // 2
+            passes = PART_PASSES
+            grouped[item] = wg_pool.tile([P, passes, FEATURES, PACK], BF16, name="w_grouped", align_bytes=64)
+            half = passes // 2
             nc.vector.tensor_copy(
                 out=grouped[item][:, 0:half].rearrange("p g (c i) t -> p g c t i", i=4),
                 in_=raw[item][:, 0:half].rearrange("p g t (c i) -> p g c t i", i=4),
             )
-            for g in range(half, PART_PASSES):
+            for g in range(half, passes):
                 nc.scalar.copy(
                     out=grouped[item][:, g].rearrange("p (c i) t -> p c t i", i=4),
                     in_=raw[item][:, g].rearrange("p t (c i) -> p c t i", i=4),
                 )
 
         def quantise_w(item):
-            w_codes[item] = wq_pool.tile([P, PART_PASSES * FEATURES], U32, name="w_codes", align_bytes=64)
-            w_scales[item] = wq_pool.tile([P, PART_PASSES * FEATURES], U8, name="w_scales", align_bytes=64)
+            columns = PART_PASSES * FEATURES
+            w_codes[item] = wq_pool.tile([P, columns], U32, name="w_codes", align_bytes=64)
+            w_scales[item] = wq_pool.tile([P, columns], U8, name="w_scales", align_bytes=64)
             nc.vector.quantize_mx(
                 out=w_codes[item][:].bitcast(FP8X4),
                 scales=w_scales[item][:],
@@ -194,26 +186,29 @@ def tile_bertheading_pa_k_kernel(tc, words_emb, W1, b1, W2, b2, W3, b3, out_0, o
                     rest[part, s] = bank_pool.tile([P, REST], F32, tag="bank", name="rest_last")
                 rest_out = rest[part, s][:]
             shift = tap * SENTENCES
-            for g in range(PART_PASSES):
+            last_tap = part == PARTS - 1 and i == len(taps) - 1
+            passes = [(g, narrow) for g in range(PART_PASSES) for narrow in (False, True)]
+            for g, narrow in sorted(passes, key=lambda each: each[1]) if last_tap else passes:
                 k_pass = part * PART_PASSES + g
                 cols = slice(g * FEATURES, (g + 1) * FEATURES)
                 opens, closes = tap == 0 and g == 0, tap == width - 1 and g == PART_PASSES - 1
-                for out, tokens, start, stop in (
-                    (main[s][:], slice(shift, shift + MAIN), opens and part == 0, closes and part == PARTS - 1),
-                    (rest_out, slice(shift + MAIN, shift + TOKENS), opens, closes),
-                ):
-                    scales = x_scales[:, k_pass, tokens]
-                    if tap == 1:
-                        scales = x_scales_moved[:, k_pass, tokens.start - shift : tokens.stop - shift]
-                    nc.tensor.matmul_mx(
-                        out=out,
-                        lhsT=w_codes[item][:, cols].bitcast(FP8X4),
-                        lhsT_scale=w_scales[item][:, cols],
-                        rhs=x_codes[:, k_pass, tokens].bitcast(FP8X4),
-                        rhs_scale=scales,
-                        start=start,
-                        stop=stop,
-                    )
+                if narrow:
+                    out, tokens, start, stop = rest_out, slice(shift + MAIN, shift + TOKENS), opens, closes
+                else:
+                    out, tokens = main[s][:], slice(shift, shift + MAIN)
+                    start, stop = opens and part == 0, closes and part == PARTS - 1
+                scales = x_scales[:, k_pass, tokens]
+                if tap == 1:
+                    scales = x_scales_moved[:, k_pass, tokens.start - shift : tokens.stop - shift]
+                nc.tensor.matmul_mx(
+                    out=out,
+                    lhsT=w_codes[item][:, cols].bitcast(FP8X4),
+                    lhsT_scale=w_scales[item][:, cols],
+                    rhs=x_codes[:, k_pass, tokens].bitcast(FP8X4),
+                    rhs_scale=scales,
+                    start=start,
+                    stop=stop,
+                )
 
         def add_rest(part):
             base = bias[:].unsqueeze(2).to_broadcast([P, len(WIDTHS), REST]) if part == 0 else rest_sum[:]
@@ -224,7 +219,8 @@ def tile_bertheading_pa_k_kernel(tc, words_emb, W1, b1, W2, b2, W3, b3, out_0, o
 
         def finish_main(width, lo, hi):
             s = WIDTHS.index(width)
-            nc.scalar.activation(out=conv[width][:, lo:hi], in_=main[s][:, lo:hi], func=ACT.Identity, bias=bias[:, s : s + 1])
+            func = ACT.Relu if width == 1 else ACT.Identity
+            nc.scalar.activation(out=conv[width][:, lo:hi], in_=main[s][:, lo:hi], func=func, bias=bias[:, s : s + 1])
 
         def finish_rest(width):
             s = WIDTHS.index(width)
@@ -236,10 +232,8 @@ def tile_bertheading_pa_k_kernel(tc, words_emb, W1, b1, W2, b2, W3, b3, out_0, o
                 op=ALU.add,
             )
 
-        def raise_code(width, lo, hi):
-            nc.vector.scalar_tensor_tensor(
-                out=code[:, lo:hi], in0=conv[width][:, lo:hi], scalar=0.0, in1=code[:, lo:hi], op0=ALU.max, op1=ALU.max
-            )
+        def raise_code(width, base, lo, hi):
+            nc.vector.tensor_tensor(out=code[:, lo:hi], in0=conv[width][:, lo:hi], in1=base[:, lo:hi], op=ALU.max)
 
         def take_peak(width):
             own = conv[width][:, 0 : own_tokens(width)].rearrange("c (p n) -> c n p", n=SENTENCES)
@@ -251,67 +245,87 @@ def tile_bertheading_pa_k_kernel(tc, words_emb, W1, b1, W2, b2, W3, b3, out_0, o
             if part < PARTS - 1:
                 if i == len(taps) - 1:
                     add_rest(part)
-            elif width > 1 and tap == width - 1:
-                conv[width] = code if width == 3 else keep.tile([P, TOKENS], F32, name="conv_2")
+            elif width < 3 and tap == width - 1:
+                conv[width] = keep.tile([P, TOKENS], F32, name=f"conv_{width}")
                 finish_main(width, 0, MAIN)
                 finish_rest(width)
-                if width == 2:
-                    raise_code(width, 0, own_tokens(width))
-                take_peak(width)
+                if width == 1:
+                    nc.scalar.activation(out=conv[1][:, MAIN:], in_=conv[1][:, MAIN:], func=ACT.Relu)
+                    nc.scalar.copy(out=code[:, own_tokens(2) :], in_=conv[1][:, own_tokens(2) :])
+                    take_peak(1)
+                else:
+                    raise_code(2, conv[1], 0, own_tokens(2))
 
         loaded = LOADS_AHEAD
-        for step in range(steps + 2):
+        for step in range(steps + MULTIPLY_LAG):
             now_x, now_w = (x_steps[step], w_steps[step]) if step < steps else ([], [])
-            last_x, last_w = (x_steps[step - 1], w_steps[step - 1]) if 1 <= step <= steps else ([], [])
-            ready_w = w_steps[step - 2] if step >= 2 else []
-            done_w = w_steps[step - 3] if step >= 3 else []
+            last_x = x_steps[step - 1] if 1 <= step <= steps else []
+            ready_w, done_w = (w_steps[step - lag] if lag <= step else [] for lag in (MULTIPLY_LAG, MULTIPLY_LAG + 1))
             for item in now_x:
                 transpose_x(item)
+            for item in ready_w:
+                multiply(item)
             for item in done_w:
                 if item[1] < PARTS - 1:
                     after_multiply(item)
-            for item in now_w[:1]:
+            for item in now_w:
                 regroup(item)
             for item in now_x:
                 copy_x(item)
-            for item in now_w[1:]:
-                regroup(item)
             for item in load_order[loaded : loaded + len(now_x) + len(now_w)]:
                 load(item)
             loaded += len(now_x) + len(now_w)
-            for part in sorted({item[1] for item in last_x}):
-                tiles = [item[2] for item in last_x if item[1] == part]
-                quantise_x(part, tiles[0] * P, (tiles[-1] + 1) * P)
-            for item in last_w:
+            for kind, part, tt in last_x:
+                if tt == TOKEN_TILES - 1:
+                    quantise_x(part, tt * P, TOKENS)
+                    move_scales(part)
+                elif tt % 2 == 1:
+                    quantise_x(part, (tt - 1) * P, (tt + 1) * P)
+            for item in now_w:
                 quantise_w(item)
-            for item in last_x:
-                if item[2] == TOKEN_TILES - 1:
-                    move_scales(item[1])
             for item in done_w:
                 if item[1] == PARTS - 1:
                     after_multiply(item)
-            for item in ready_w:
-                multiply(item)
-            if step == W_START:
+            if step == TOKEN_TILES:
                 bias_rows_f32 = keep.tile([P, P], F32)
                 nc.vector.tensor_copy(out=bias_rows_f32[:], in_=bias_rows[:])
                 bias_bank = bank_pool.tile([P, P], F32, tag="bank")
                 nc.tensor.transpose(bias_bank[:], bias_rows_f32[:], ident[:])
                 nc.vector.tensor_copy(out=bias[:], in_=bias_bank[:, 0 : len(WIDTHS)])
 
+        fold_column = keep.tile([P, BLOCK], F32)
+        nc.vector.tensor_reduce(
+            out=fold_column[:], in_=ident[:].rearrange("i (b n) -> i n b", n=BLOCK), axis=AXIS.X, op=ALU.add
+        )
+        fold = keep.tile([P, P], F32)
+        nc.vector.tensor_copy(
+            out=fold[:].rearrange("i (b n) -> i b n", n=BLOCK),
+            in_=fold_column[:].unsqueeze(1).to_broadcast([P, P // BLOCK, BLOCK]),
+        )
+        take_peak(2)
+        third = keep.tile([P, len(WIDTHS), SENTENCES], F32)
+        first_two = keep.tile([P, SENTENCES], F32)
+        nc.gpsimd.tensor_scalar(
+            out=third[:, 0:2, :], in0=peak[:, 0:2, :], scalar1=0.0, scalar2=1.0 / 3.0, op0=ALU.max, op1=ALU.mult
+        )
+        nc.gpsimd.tensor_tensor(out=first_two[:], in0=third[:, 0, :], in1=third[:, 1, :], op=ALU.add)
+
         pieces = [slice(i * P, (i + 1) * P) for i in range(TOKEN_TILES)]
-        conv[1] = keep.tile([P, TOKENS], F32, name="conv_1")
+        conv[3] = keep.tile([P, TOKENS], F32, name="conv_3")
         code_t = keep.tile([P, TOKENS], F32, align_bytes=64)
         squares_t = keep.tile([P, TOKENS], F32)
         part_norm = keep.tile([P, POSITIONS], F32)
         for i in range(MAIN // P):
-            finish_main(1, i * P, (i + 1) * P)
-        finish_rest(1)
-        for i in range(TOKEN_TILES + 1):
-            if i < TOKEN_TILES:
-                raise_code(1, i * P, (i + 1) * P)
-            if i >= 1:
-                nc.vector.transpose(out=code_t[:, pieces[i - 1]], in_=code[:, pieces[i - 1]])
+            finish_main(3, i * P, (i + 1) * P)
+        for i in range(TOKEN_TILES + 2):
+            if i == TOKEN_TILES - 1:
+                finish_rest(3)
+            elif i < TOKEN_TILES + 1:
+                j = min(i, TOKEN_TILES - 1)
+                raise_code(3, code, j * P, min((j + 1) * P, own_tokens(3)))
+            if i >= 1 and i != TOKEN_TILES:
+                j = min(i - 1, TOKEN_TILES - 1)
+                nc.vector.transpose(out=code_t[:, pieces[j]], in_=code[:, pieces[j]])
         for cols in pieces:
             nc.scalar.activation(out=squares_t[:, cols], in_=code_t[:, cols], func=ACT.Square)
         for i, cols in enumerate(pieces):
@@ -323,28 +337,28 @@ def tile_bertheading_pa_k_kernel(tc, words_emb, W1, b1, W2, b2, W3, b3, out_0, o
             )
         norm_bank = bank_pool.tile([P, POSITIONS], F32, tag="bank")
         nc.tensor.matmul(out=norm_bank[:], lhsT=fold[:], rhs=part_norm[:], start=True, stop=True)
-        take_peak(1)
+        take_peak(3)
         inv_norm = keep.tile([P, POSITIONS], F32)
         nc.scalar.activation(out=inv_norm[:], in_=norm_bank[:], func=ACT.Abs_reciprocal_sqrt)
+        nc.gpsimd.tensor_scalar(
+            out=third[:, 2, :], in0=peak[:, 2, :], scalar1=0.0, scalar2=1.0 / 3.0, op0=ALU.max, op1=ALU.mult
+        )
+        nc.gpsimd.tensor_tensor(out=pooled_cn[:, 0:SENTENCES], in0=first_two[:], in1=third[:, 2, :], op=ALU.add)
+        pooled_bank = bank_pool.tile([P, P], F32, tag="bank")
+        nc.tensor.transpose(pooled_bank[:], pooled_cn[:], ident[:])
+        pooled_nc = keep.tile([SENTENCES, FEATURES], F32)
+        nc.scalar.copy(out=pooled_nc[:], in_=pooled_bank[0:SENTENCES, :])
+        nc.scalar.dma_start(out=out_1[:, :], in_=pooled_nc[:])
         words = keep.tile([P, BLOCK, POSITIONS], F32)
-        nc.vector.scalar_tensor_tensor(
-            out=words[:],
-            in0=inv_norm[:].unsqueeze(1).to_broadcast([P, BLOCK, POSITIONS]),
-            scalar=1.0e12,
-            in1=code_t[:].rearrange("q (p c) -> q c p", c=BLOCK),
-            op0=ALU.min,
-            op1=ALU.mult,
+        nc.vector.tensor_scalar_min(inv_norm[:], inv_norm[:], 1.0e12)
+        nc.vector.tensor_tensor(
+            out=words[:].rearrange("q c (g i) -> q g c i", i=4),
+            in0=inv_norm[:].rearrange("q (g i) -> q g i", i=4).unsqueeze(2).to_broadcast([P, POSITIONS // 4, BLOCK, 4]),
+            in1=code_t[:].rearrange("q (g i c) -> q g c i", i=4, c=BLOCK),
+            op=ALU.mult,
         )
         for b in range(P // BLOCK):
             nc.sync.dma_start(
                 out=out_0[:, b * BLOCK : (b + 1) * BLOCK, :].rearrange("n c p -> n (c p)"),
                 in_=words[b * BLOCK : (b + 1) * BLOCK].rearrange("q c p -> q (c p)"),
             )
-
-        nc.vector.tensor_scalar(out=peak[:], in0=peak[:], scalar1=0.0, scalar2=1.0 / 3.0, op0=ALU.max, op1=ALU.mult)
-        pooled_cn = keep.tile([P, SENTENCES], F32, align_bytes=64)
-        nc.vector.tensor_reduce(out=pooled_cn[:], in_=peak[:].rearrange("c k n -> c n k"), axis=AXIS.X, op=ALU.add)
-        pooled_t = keep.tile([P, BLOCK], F32, align_bytes=64)
-        nc.vector.transpose(out=pooled_t[:], in_=pooled_cn[:])
-        for b in range(P // BLOCK):
-            nc.sync.dma_start(out=out_1[:, b * BLOCK : (b + 1) * BLOCK], in_=pooled_t[b * BLOCK : (b + 1) * BLOCK, :])

@@ -28,6 +28,7 @@ PAD = (max(WIDTHS) - 1) * SENTENCES
 
 TILE_POSITIONS = P // SENTENCES
 PART_PASSES = 4
+LAST_PASSES = 2
 PARTS = PASSES // PART_PASSES
 BANK_PASSES = 2
 MULTIPLY_LAG = 2
@@ -48,7 +49,7 @@ def tile_bertheading_pa_k_kernel(tc, words_emb, W1, b1, W2, b2, W3, b3, out_0, o
         w_pool = stack.enter_context(tc.tile_pool(name="w_pool", bufs=12))
         wg_pool = stack.enter_context(tc.tile_pool(name="wg_pool", bufs=3))
         wq_pool = stack.enter_context(tc.tile_pool(name="wq_pool", bufs=6))
-        bank_pool = stack.enter_context(tc.psum_pool(name="bank_pool", bufs=4))
+        bank_pool = stack.enter_context(tc.psum_pool(name="bank_pool", bufs=2))
         acc_pool = stack.enter_context(tc.psum_pool(name="acc_pool", bufs=1))
 
         warm = keep.tile([P, 1], F32)
@@ -66,31 +67,42 @@ def tile_bertheading_pa_k_kernel(tc, words_emb, W1, b1, W2, b2, W3, b3, out_0, o
         nc.vector.tensor_copy(
             out=perm[:].rearrange("i (a n) -> i a n", n=SENTENCES), in_=ident[:].rearrange("i (n a) -> i a n", n=SENTENCES)
         )
+        fold_column = keep.tile([P, BLOCK], F32)
+        nc.vector.tensor_reduce(
+            out=fold_column[:], in_=ident[:].rearrange("i (b n) -> i n b", n=BLOCK), axis=AXIS.X, op=ALU.add
+        )
+        fold = keep.tile([P, P], F32)
+        nc.vector.tensor_copy(
+            out=fold[:].rearrange("i (b n) -> i b n", n=BLOCK),
+            in_=fold_column[:].unsqueeze(1).to_broadcast([P, P // BLOCK, BLOCK]),
+        )
         x_codes = keep.tile([P, PASSES, TOKENS + PAD], U32, align_bytes=64)
         x_scales = keep.tile([P, PASSES, TOKENS + PAD], U8, align_bytes=64)
         x_scales_moved = keep.tile([P, PASSES, TOKENS], U8, align_bytes=64)
         nc.gpsimd.memset(x_codes[:, :, TOKENS:], 0)
         nc.gpsimd.memset(x_scales[:].bitcast(I32), 0)
         code = keep.tile([P, TOKENS], F32, align_bytes=64)
-        pooled_cn = keep.tile([P, P], F32)
+        pooled_cn = keep.tile([P, len(WIDTHS) - 1 + P // SENTENCES, SENTENCES], F32)
         nc.gpsimd.memset(pooled_cn[:], 0.0)
 
         taps = [(width, tap) for width in WIDTHS for tap in range(width)]
         weights = {3: W3, 2: W2, 1: W1}
-        x_steps = [[("x", 0, tt)] for tt in range(TOKEN_TILES)]
-        w_steps = [[] for step in x_steps]
-        for part in range(PARTS):
-            for i in range(len(taps)):
-                x_steps.append([("x", part + 1, i)] if i < TOKEN_TILES and part + 1 < PARTS else [])
-                w_steps.append([("w", part, i)])
-        steps = len(w_steps)
+        x_items = [("x", part * PART_PASSES, PART_PASSES, tt) for part in range(PARTS) for tt in range(TOKEN_TILES)]
+        w_items = [("w", part * PART_PASSES, PART_PASSES, i) for part in range(PARTS) for i in range(len(taps))]
+        kind, first, passes, i = w_items.pop()
+        w_items += [(kind, k, LAST_PASSES, i) for k in range(first, first + passes, LAST_PASSES)]
+        x_steps = []
+        for item in x_items:
+            x_steps += [[item], []] if item[1] > 0 and item[3] == TOKEN_TILES - 1 else [[item]]
+        w_steps = [[] for tt in range(TOKEN_TILES - 1)] + [[item] for item in w_items]
+        steps = max(len(x_steps), len(w_steps))
+        x_steps += [[]] * (steps - len(x_steps))
         load_order = [item for step in range(steps) for item in x_steps[step] + w_steps[step]]
         raw, grouped, x_grouped, banks, w_codes, w_scales = {}, {}, {}, {}, {}, {}
 
         def load(item):
-            kind, part, i = item
-            passes = PART_PASSES
-            rows = slice(part * PART_PASSES * K_PASS, (part * PART_PASSES + passes) * K_PASS)
+            kind, first, passes, i = item
+            rows = slice(first * K_PASS, (first + passes) * K_PASS)
             if kind == "x":
                 raw[item] = x_pool.tile([P, passes * K_PASS], BF16, name="x_raw")
                 src = words_emb[:, i * TILE_POSITIONS : (i + 1) * TILE_POSITIONS, rows]
@@ -104,67 +116,63 @@ def tile_bertheading_pa_k_kernel(tc, words_emb, W1, b1, W2, b2, W3, b3, out_0, o
             load(item)
 
         bias = keep.tile([P, len(WIDTHS)], F32)
-        peak = keep.tile([P, len(WIDTHS), SENTENCES], F32)
-        main = [acc_pool.tile([P, MAIN], F32, name=f"main_{width}") for width in WIDTHS]
-        rest_sum = keep.tile([P, len(WIDTHS), REST], F32)
-        rest = {}
-        conv = {}
+        peak = keep.tile([P, len(WIDTHS), 2, SENTENCES], F32)
+        main, rest = {}, {}
 
         def transpose_x(item):
-            part, tt = item[1:]
+            kind, first, passes, tt = item
             if tt == 0:
-                x_grouped[part] = xg_pool.tile([P, PART_PASSES, TOKENS, PACK], BF16, name="x_grouped", align_bytes=64)
+                x_grouped[first] = xg_pool.tile([P, passes, TOKENS, PACK], BF16, name="x_grouped", align_bytes=64)
             x_words = raw[item][:].bitcast(F32).rearrange("r (g p u) -> r g u p", p=P, u=2)
-            for j in range(PART_PASSES // BANK_PASSES):
-                first = j * BANK_PASSES
-                bank = bank_pool.tile([P, BANK_PASSES, 2, P], F32, tag="bank")
+            for j in range(passes // BANK_PASSES):
+                shape = [P, BANK_PASSES, 2, P]
+                if first == 0 and tt in (1, 2):
+                    bank = acc_pool.tile(shape, F32, name="borrowed", tag=f"{('main', 'rest')[j]}_{tt + 1}")
+                else:
+                    bank = bank_pool.tile(shape, F32, tag="bank")
                 banks[item, j] = bank
                 for g in range(BANK_PASSES):
                     for u in range(2):
-                        nc.tensor.transpose(bank[:, g, u, :], x_words[:, first + g, u, :], perm[:])
+                        nc.tensor.transpose(bank[:, g, u, :], x_words[:, j * BANK_PASSES + g, u, :], perm[:])
 
         def copy_x(item):
-            part, tt = item[1:]
-            grouped_words = x_grouped[part][:].rearrange("p g r t -> p (g r t)").bitcast(F32)
+            kind, first, passes, tt = item
+            grouped_words = x_grouped[first][:].rearrange("p g r t -> p (g r t)").bitcast(F32)
             grouped_words = grouped_words.rearrange("p (g r u) -> p g r u", r=TOKENS, u=2)
-            for j in range(PART_PASSES // BANK_PASSES):
-                first = j * BANK_PASSES
+            for j in range(passes // BANK_PASSES):
                 nc.scalar.copy(
-                    out=grouped_words[:, first : first + BANK_PASSES, tt * P : (tt + 1) * P, :],
+                    out=grouped_words[:, j * BANK_PASSES : (j + 1) * BANK_PASSES, tt * P : (tt + 1) * P, :],
                     in_=banks[item, j][:].rearrange("p g u r -> p g r u"),
                 )
 
-        def quantise_x(part, first, last):
-            for g in range(PART_PASSES):
-                k_pass = part * PART_PASSES + g
+        def quantise_x(item):
+            kind, first, passes, tt = item
+            if tt % 2 == 0 and tt < TOKEN_TILES - 1:
+                return
+            tokens = slice(tt // 2 * 2 * P, (tt + 1) * P)
+            for g in range(passes):
                 nc.vector.quantize_mx(
-                    out=x_codes[:, k_pass, first:last].bitcast(FP8X4),
-                    scales=x_scales[:, k_pass, first:last],
-                    in_=x_grouped[part][:, g, first:last, :].rearrange("p r t -> p (r t)"),
+                    out=x_codes[:, first + g, tokens].bitcast(FP8X4),
+                    scales=x_scales[:, first + g, tokens],
+                    in_=x_grouped[first][:, g, tokens, :].rearrange("p r t -> p (r t)"),
+                )
+            if tt == TOKEN_TILES - 1:
+                ks = slice(first, first + passes)
+                nc.vector.tensor_copy(
+                    out=x_scales_moved[:, ks, :].bitcast(I32), in_=x_scales[:, ks, SENTENCES : SENTENCES + TOKENS].bitcast(I32)
                 )
 
-        def move_scales(part):
-            ks = slice(part * PART_PASSES, part * PART_PASSES + PART_PASSES)
-            nc.vector.tensor_copy(
-                out=x_scales_moved[:, ks, :].bitcast(I32), in_=x_scales[:, ks, SENTENCES : SENTENCES + TOKENS].bitcast(I32)
-            )
-
         def regroup(item):
-            passes = PART_PASSES
+            passes = item[2]
             grouped[item] = wg_pool.tile([P, passes, FEATURES, PACK], BF16, name="w_grouped", align_bytes=64)
-            half = passes // 2
-            nc.vector.tensor_copy(
-                out=grouped[item][:, 0:half].rearrange("p g (c i) t -> p g c t i", i=4),
-                in_=raw[item][:, 0:half].rearrange("p g t (c i) -> p g c t i", i=4),
-            )
-            for g in range(half, passes):
-                nc.scalar.copy(
-                    out=grouped[item][:, g].rearrange("p (c i) t -> p c t i", i=4),
-                    in_=raw[item][:, g].rearrange("p t (c i) -> p c t i", i=4),
+            for copy, half in ((nc.vector.tensor_copy, slice(0, passes // 2)), (nc.scalar.copy, slice(passes // 2, passes))):
+                copy(
+                    out=grouped[item][:, half].rearrange("p g (c i) t -> p g c t i", i=4),
+                    in_=raw[item][:, half].rearrange("p g t (c i) -> p g c t i", i=4),
                 )
 
         def quantise_w(item):
-            columns = PART_PASSES * FEATURES
+            columns = item[2] * FEATURES
             w_codes[item] = wq_pool.tile([P, columns], U32, name="w_codes", align_bytes=64)
             w_scales[item] = wq_pool.tile([P, columns], U8, name="w_scales", align_bytes=64)
             nc.vector.quantize_mx(
@@ -174,29 +182,20 @@ def tile_bertheading_pa_k_kernel(tc, words_emb, W1, b1, W2, b2, W3, b3, out_0, o
             )
 
         def multiply(item):
-            part, i = item[1:]
+            kind, first, passes, i = item
             width, tap = taps[i]
-            s = WIDTHS.index(width)
-            if part < PARTS - 1:
-                if i == 0:
-                    rest[part] = acc_pool.tile([P, len(WIDTHS), REST], F32, name="rest")
-                rest_out = rest[part][:, s, :]
-            else:
-                if tap == 0:
-                    rest[part, s] = bank_pool.tile([P, REST], F32, tag="bank", name="rest_last")
-                rest_out = rest[part, s][:]
+            if first == 0 and tap == 0:
+                main[width] = acc_pool.tile([P, MAIN], F32, name=f"main_{width}")
+                rest[width] = acc_pool.tile([P, MAIN], F32, name=f"rest_{width}")
             shift = tap * SENTENCES
-            last_tap = part == PARTS - 1 and i == len(taps) - 1
-            passes = [(g, narrow) for g in range(PART_PASSES) for narrow in (False, True)]
-            for g, narrow in sorted(passes, key=lambda each: each[1]) if last_tap else passes:
-                k_pass = part * PART_PASSES + g
+            order = [(g, narrow) for g in range(passes) for narrow in (False, True)]
+            for g, narrow in sorted(order, key=lambda each: each[1]) if item == w_items[-1] else order:
+                k_pass = first + g
                 cols = slice(g * FEATURES, (g + 1) * FEATURES)
-                opens, closes = tap == 0 and g == 0, tap == width - 1 and g == PART_PASSES - 1
                 if narrow:
-                    out, tokens, start, stop = rest_out, slice(shift + MAIN, shift + TOKENS), opens, closes
+                    out, tokens = rest[width][:, 0:REST], slice(shift + MAIN, shift + TOKENS)
                 else:
-                    out, tokens = main[s][:], slice(shift, shift + MAIN)
-                    start, stop = opens and part == 0, closes and part == PARTS - 1
+                    out, tokens = main[width][:], slice(shift, shift + MAIN)
                 scales = x_scales[:, k_pass, tokens]
                 if tap == 1:
                     scales = x_scales_moved[:, k_pass, tokens.start - shift : tokens.stop - shift]
@@ -206,55 +205,39 @@ def tile_bertheading_pa_k_kernel(tc, words_emb, W1, b1, W2, b2, W3, b3, out_0, o
                     lhsT_scale=w_scales[item][:, cols],
                     rhs=x_codes[:, k_pass, tokens].bitcast(FP8X4),
                     rhs_scale=scales,
-                    start=start,
-                    stop=stop,
+                    start=(tap == 0 and k_pass == 0),
+                    stop=(tap == width - 1 and k_pass == PASSES - 1),
                 )
-
-        def add_rest(part):
-            base = bias[:].unsqueeze(2).to_broadcast([P, len(WIDTHS), REST]) if part == 0 else rest_sum[:]
-            nc.vector.tensor_tensor(out=rest_sum[:], in0=rest[part][:], in1=base, op=ALU.add)
 
         def own_tokens(width):
             return (POSITIONS - width + 1) * SENTENCES
 
-        def finish_main(width, lo, hi):
-            s = WIDTHS.index(width)
-            func = ACT.Relu if width == 1 else ACT.Identity
-            nc.scalar.activation(out=conv[width][:, lo:hi], in_=main[s][:, lo:hi], func=func, bias=bias[:, s : s + 1])
+        def sums(width, lo, hi):
+            return main[width][:, lo:hi] if hi <= MAIN else rest[width][:, lo - MAIN : hi - MAIN]
 
-        def finish_rest(width):
-            s = WIDTHS.index(width)
-            hi = own_tokens(width)
-            nc.vector.tensor_tensor(
-                out=conv[width][:, MAIN:hi],
-                in0=rest[PARTS - 1, s][:, 0 : hi - MAIN],
-                in1=rest_sum[:, s, 0 : hi - MAIN],
-                op=ALU.add,
+        def bias_of(width):
+            return bias[:, WIDTHS.index(width) : WIDTHS.index(width) + 1]
+
+        def raise_code(width, lo, hi):
+            nc.vector.scalar_tensor_tensor(
+                out=code[:, lo:hi], in0=sums(width, lo, hi), scalar=bias_of(width), in1=code[:, lo:hi], op0=ALU.add, op1=ALU.max
             )
 
-        def raise_code(width, base, lo, hi):
-            nc.vector.tensor_tensor(out=code[:, lo:hi], in0=conv[width][:, lo:hi], in1=base[:, lo:hi], op=ALU.max)
-
         def take_peak(width):
-            own = conv[width][:, 0 : own_tokens(width)].rearrange("c (p n) -> c n p", n=SENTENCES)
-            nc.vector.tensor_reduce(out=peak[:, WIDTHS.index(width), :], in_=own, axis=AXIS.X, op=ALU.max)
+            for h, (lo, hi) in enumerate(((0, MAIN), (MAIN, own_tokens(width)))):
+                by_sentence = sums(width, lo, hi).rearrange("c (p n) -> c n p", n=SENTENCES)
+                nc.vector.tensor_reduce(out=peak[:, WIDTHS.index(width), h, :], in_=by_sentence, axis=AXIS.X, op=ALU.max)
 
         def after_multiply(item):
-            part, i = item[1:]
-            width, tap = taps[i]
-            if part < PARTS - 1:
-                if i == len(taps) - 1:
-                    add_rest(part)
-            elif width < 3 and tap == width - 1:
-                conv[width] = keep.tile([P, TOKENS], F32, name=f"conv_{width}")
-                finish_main(width, 0, MAIN)
-                finish_rest(width)
-                if width == 1:
-                    nc.scalar.activation(out=conv[1][:, MAIN:], in_=conv[1][:, MAIN:], func=ACT.Relu)
-                    nc.scalar.copy(out=code[:, own_tokens(2) :], in_=conv[1][:, own_tokens(2) :])
-                    take_peak(1)
-                else:
-                    raise_code(2, conv[1], 0, own_tokens(2))
+            kind, first, passes, i = item
+            if first + passes < PASSES:
+                return
+            if taps[i] == (1, 0):
+                for lo, hi in ((0, MAIN), (MAIN, TOKENS)):
+                    nc.scalar.activation(out=code[:, lo:hi], in_=sums(1, lo, hi), func=ACT.Relu, bias=bias_of(1))
+            elif taps[i] == (2, 1):
+                raise_code(2, 0, MAIN)
+                raise_code(2, MAIN, own_tokens(2))
 
         loaded = LOADS_AHEAD
         for step in range(steps + MULTIPLY_LAG):
@@ -263,11 +246,14 @@ def tile_bertheading_pa_k_kernel(tc, words_emb, W1, b1, W2, b2, W3, b3, out_0, o
             ready_w, done_w = (w_steps[step - lag] if lag <= step else [] for lag in (MULTIPLY_LAG, MULTIPLY_LAG + 1))
             for item in now_x:
                 transpose_x(item)
+            if step == 1:
+                bias_rows_f32 = keep.tile([P, P], F32)
+                nc.vector.tensor_copy(out=bias_rows_f32[:], in_=bias_rows[:])
+                bias_bank = bank_pool.tile([P, P], F32, tag="bank")
+                nc.tensor.transpose(bias_bank[:], bias_rows_f32[:], ident[:])
+                nc.vector.tensor_copy(out=bias[:], in_=bias_bank[:, 0 : len(WIDTHS)])
             for item in ready_w:
                 multiply(item)
-            for item in done_w:
-                if item[1] < PARTS - 1:
-                    after_multiply(item)
             for item in now_w:
                 regroup(item)
             for item in now_x:
@@ -275,79 +261,60 @@ def tile_bertheading_pa_k_kernel(tc, words_emb, W1, b1, W2, b2, W3, b3, out_0, o
             for item in load_order[loaded : loaded + len(now_x) + len(now_w)]:
                 load(item)
             loaded += len(now_x) + len(now_w)
-            for kind, part, tt in last_x:
-                if tt == TOKEN_TILES - 1:
-                    quantise_x(part, tt * P, TOKENS)
-                    move_scales(part)
-                elif tt % 2 == 1:
-                    quantise_x(part, (tt - 1) * P, (tt + 1) * P)
+            for item in last_x:
+                quantise_x(item)
             for item in now_w:
                 quantise_w(item)
             for item in done_w:
-                if item[1] == PARTS - 1:
-                    after_multiply(item)
-            if step == TOKEN_TILES:
-                bias_rows_f32 = keep.tile([P, P], F32)
-                nc.vector.tensor_copy(out=bias_rows_f32[:], in_=bias_rows[:])
-                bias_bank = bank_pool.tile([P, P], F32, tag="bank")
-                nc.tensor.transpose(bias_bank[:], bias_rows_f32[:], ident[:])
-                nc.vector.tensor_copy(out=bias[:], in_=bias_bank[:, 0 : len(WIDTHS)])
+                after_multiply(item)
 
-        fold_column = keep.tile([P, BLOCK], F32)
-        nc.vector.tensor_reduce(
-            out=fold_column[:], in_=ident[:].rearrange("i (b n) -> i n b", n=BLOCK), axis=AXIS.X, op=ALU.add
-        )
-        fold = keep.tile([P, P], F32)
-        nc.vector.tensor_copy(
-            out=fold[:].rearrange("i (b n) -> i b n", n=BLOCK),
-            in_=fold_column[:].unsqueeze(1).to_broadcast([P, P // BLOCK, BLOCK]),
-        )
-        take_peak(2)
-        third = keep.tile([P, len(WIDTHS), SENTENCES], F32)
-        first_two = keep.tile([P, SENTENCES], F32)
-        nc.gpsimd.tensor_scalar(
-            out=third[:, 0:2, :], in0=peak[:, 0:2, :], scalar1=0.0, scalar2=1.0 / 3.0, op0=ALU.max, op1=ALU.mult
-        )
-        nc.gpsimd.tensor_tensor(out=first_two[:], in0=third[:, 0, :], in1=third[:, 1, :], op=ALU.add)
+        take_peak(1)
 
-        pieces = [slice(i * P, (i + 1) * P) for i in range(TOKEN_TILES)]
-        conv[3] = keep.tile([P, TOKENS], F32, name="conv_3")
         code_t = keep.tile([P, TOKENS], F32, align_bytes=64)
         squares_t = keep.tile([P, TOKENS], F32)
         part_norm = keep.tile([P, POSITIONS], F32)
-        for i in range(MAIN // P):
-            finish_main(3, i * P, (i + 1) * P)
-        for i in range(TOKEN_TILES + 2):
-            if i == TOKEN_TILES - 1:
-                finish_rest(3)
-            elif i < TOKEN_TILES + 1:
-                j = min(i, TOKEN_TILES - 1)
-                raise_code(3, code, j * P, min((j + 1) * P, own_tokens(3)))
-            if i >= 1 and i != TOKEN_TILES:
-                j = min(i - 1, TOKEN_TILES - 1)
-                nc.vector.transpose(out=code_t[:, pieces[j]], in_=code[:, pieces[j]])
+        pieces = [slice(0, MAIN // 2), slice(MAIN // 2, MAIN), slice(MAIN, TOKENS)]
+
+        def turn(cols):
+            nc.vector.transpose(out=code_t[:, cols], in_=code[:, cols])
+
+        raise_code(3, 0, MAIN // 2)
+        raise_code(3, MAIN // 2, MAIN)
+        turn(pieces[0])
+        raise_code(3, MAIN, own_tokens(3))
+        turn(pieces[1])
+        turn(pieces[2])
         for cols in pieces:
             nc.scalar.activation(out=squares_t[:, cols], in_=code_t[:, cols], func=ACT.Square)
-        for i, cols in enumerate(pieces):
+        for cols in pieces:
             nc.vector.tensor_reduce(
-                out=part_norm[:, i * TILE_POSITIONS : (i + 1) * TILE_POSITIONS],
+                out=part_norm[:, cols.start // SENTENCES : cols.stop // SENTENCES],
                 in_=squares_t[:, cols].rearrange("q (p c) -> q p c", c=BLOCK),
                 axis=AXIS.X,
                 op=ALU.add,
             )
         norm_bank = bank_pool.tile([P, POSITIONS], F32, tag="bank")
         nc.tensor.matmul(out=norm_bank[:], lhsT=fold[:], rhs=part_norm[:], start=True, stop=True)
+        take_peak(2)
         take_peak(3)
         inv_norm = keep.tile([P, POSITIONS], F32)
         nc.scalar.activation(out=inv_norm[:], in_=norm_bank[:], func=ACT.Abs_reciprocal_sqrt)
-        nc.gpsimd.tensor_scalar(
-            out=third[:, 2, :], in0=peak[:, 2, :], scalar1=0.0, scalar2=1.0 / 3.0, op0=ALU.max, op1=ALU.mult
-        )
-        nc.gpsimd.tensor_tensor(out=pooled_cn[:, 0:SENTENCES], in0=first_two[:], in1=third[:, 2, :], op=ALU.add)
+        top = keep.tile([P, len(WIDTHS), SENTENCES], F32)
+        nc.vector.tensor_tensor(out=top[:], in0=peak[:, :, 0, :], in1=peak[:, :, 1, :], op=ALU.max)
         pooled_bank = bank_pool.tile([P, P], F32, tag="bank")
-        nc.tensor.transpose(pooled_bank[:], pooled_cn[:], ident[:])
+        for s, width in enumerate(WIDTHS):
+            nc.scalar.activation(out=pooled_cn[:, s, :], in_=top[:, s, :], func=ACT.Relu, bias=bias_of(width))
+        pooled_columns = pooled_cn[:].rearrange("c s n -> c (s n)")
+        for s in range(len(WIDTHS)):
+            nc.tensor.matmul(
+                out=pooled_bank[:],
+                lhsT=pooled_columns[:, s * SENTENCES : s * SENTENCES + P],
+                rhs=ident[:],
+                start=(s == 0),
+                stop=(s == len(WIDTHS) - 1),
+            )
         pooled_nc = keep.tile([SENTENCES, FEATURES], F32)
-        nc.scalar.copy(out=pooled_nc[:], in_=pooled_bank[0:SENTENCES, :])
+        nc.scalar.mul(pooled_nc[:], pooled_bank[0:SENTENCES, :], 1.0 / len(WIDTHS))
         nc.scalar.dma_start(out=out_1[:, :], in_=pooled_nc[:])
         words = keep.tile([P, BLOCK, POSITIONS], F32)
         nc.vector.tensor_scalar_min(inv_norm[:], inv_norm[:], 1.0e12)

@@ -82,7 +82,7 @@ def tile_bertheading_pa_k_kernel(tc, words_emb, W1, b1, W2, b2, W3, b3, out_0, o
         nc.gpsimd.memset(x_codes[:, :, TOKENS:], 0)
         nc.gpsimd.memset(x_scales[:].bitcast(I32), 0)
         code = keep.tile([P, TOKENS], F32, align_bytes=64)
-        pooled_cn = keep.tile([P, len(WIDTHS) - 1 + P // SENTENCES, SENTENCES], F32)
+        pooled_cn = keep.tile([P, P], F32)
         nc.gpsimd.memset(pooled_cn[:], 0.0)
 
         taps = [(width, tap) for width in WIDTHS for tap in range(width)]
@@ -167,8 +167,8 @@ def tile_bertheading_pa_k_kernel(tc, words_emb, W1, b1, W2, b2, W3, b3, out_0, o
             grouped[item] = wg_pool.tile([P, passes, FEATURES, PACK], BF16, name="w_grouped", align_bytes=64)
             for copy, half in ((nc.vector.tensor_copy, slice(0, passes // 2)), (nc.scalar.copy, slice(passes // 2, passes))):
                 copy(
-                    out=grouped[item][:, half].rearrange("p g (c i) t -> p g c t i", i=4),
-                    in_=raw[item][:, half].rearrange("p g t (c i) -> p g c t i", i=4),
+                    out=grouped[item][:, half].rearrange("p g (c i) t -> p g c t i", i=8),
+                    in_=raw[item][:, half].rearrange("p g t (c i) -> p g c t i", i=8),
                 )
 
         def quantise_w(item):
@@ -301,21 +301,8 @@ def tile_bertheading_pa_k_kernel(tc, words_emb, W1, b1, W2, b2, W3, b3, out_0, o
         nc.scalar.activation(out=inv_norm[:], in_=norm_bank[:], func=ACT.Abs_reciprocal_sqrt)
         top = keep.tile([P, len(WIDTHS), SENTENCES], F32)
         nc.vector.tensor_tensor(out=top[:], in0=peak[:, :, 0, :], in1=peak[:, :, 1, :], op=ALU.max)
-        pooled_bank = bank_pool.tile([P, P], F32, tag="bank")
         for s, width in enumerate(WIDTHS):
-            nc.scalar.activation(out=pooled_cn[:, s, :], in_=top[:, s, :], func=ACT.Relu, bias=bias_of(width))
-        pooled_columns = pooled_cn[:].rearrange("c s n -> c (s n)")
-        for s in range(len(WIDTHS)):
-            nc.tensor.matmul(
-                out=pooled_bank[:],
-                lhsT=pooled_columns[:, s * SENTENCES : s * SENTENCES + P],
-                rhs=ident[:],
-                start=(s == 0),
-                stop=(s == len(WIDTHS) - 1),
-            )
-        pooled_nc = keep.tile([SENTENCES, FEATURES], F32)
-        nc.scalar.mul(pooled_nc[:], pooled_bank[0:SENTENCES, :], 1.0 / len(WIDTHS))
-        nc.scalar.dma_start(out=out_1[:, :], in_=pooled_nc[:])
+            nc.scalar.activation(out=top[:, s, :], in_=top[:, s, :], func=ACT.Relu, bias=bias_of(width))
         words = keep.tile([P, BLOCK, POSITIONS], F32)
         nc.vector.tensor_scalar_min(inv_norm[:], inv_norm[:], 1.0e12)
         nc.vector.tensor_tensor(
@@ -324,6 +311,14 @@ def tile_bertheading_pa_k_kernel(tc, words_emb, W1, b1, W2, b2, W3, b3, out_0, o
             in1=code_t[:].rearrange("q (g i c) -> q g c i", i=4, c=BLOCK),
             op=ALU.mult,
         )
+        nc.vector.tensor_reduce(
+            out=pooled_cn[:, 0:SENTENCES], in_=top[:].rearrange("c s n -> c n s"), axis=AXIS.X, op=ALU.add
+        )
+        pooled_bank = bank_pool.tile([P, P], F32, tag="bank")
+        nc.tensor.transpose(pooled_bank[:], pooled_cn[:], ident[:])
+        pooled_nc = keep.tile([SENTENCES, FEATURES], F32)
+        nc.scalar.mul(pooled_nc[:], pooled_bank[0:SENTENCES, :], 1.0 / len(WIDTHS))
+        nc.scalar.dma_start(out=out_1[:, :], in_=pooled_nc[:])
         for b in range(P // BLOCK):
             nc.sync.dma_start(
                 out=out_0[:, b * BLOCK : (b + 1) * BLOCK, :].rearrange("n c p -> n (c p)"),

from contextlib import ExitStack

import concourse.mybir as mybir
from concourse.masks import make_identity

F32 = mybir.dt.float32
BF16 = mybir.dt.bfloat16
U32 = mybir.dt.uint32
I32 = mybir.dt.int32
U8 = mybir.dt.uint8
FP8X4 = mybir.dt.float8_e4m3fn_x4
ALU = mybir.AluOpType
ACT = mybir.ActivationFunctionType
AXIS = mybir.AxisListType

P = 128
PACK = 4
K_PASS = P * PACK

SENTENCES, POSITIONS, EMBED, FEATURES = 32, 20, 8192, 128
WIDTHS = (1, 2, 3)
TOKENS = SENTENCES * POSITIONS
PASSES = EMBED // K_PASS
TOKEN_TILES = TOKENS // P
MAIN = 512
REST = TOKENS - MAIN
PAD = (max(WIDTHS) - 1) * SENTENCES

TILE_POSITIONS = P // SENTENCES
PART_PASSES = 4
LAST_PASSES = 2
PARTS = PASSES // PART_PASSES
BANK_PASSES = 2
MULTIPLY_LAG = 2
LOADS_AHEAD = 12
BLOCK = 32

FLOPS = 2 * EMBED * FEATURES * SENTENCES * (20 * 1 + 19 * 2 + 18 * 3)


def tile_bertheading_pa_k_kernel(tc, words_emb, W1, b1, W2, b2, W3, b3, out_0, out_1):
    nc = tc.nc

    with ExitStack() as stack:
        stack.enter_context(tc.manual_schedule())
        keep = stack.enter_context(tc.tile_pool(name="keep", bufs=1))
        x_pool = stack.enter_context(tc.tile_pool(name="x_pool", bufs=8))
        xg_pool = stack.enter_context(tc.tile_pool(name="xg_pool", bufs=2))
        w_pool = stack.enter_context(tc.tile_pool(name="w_pool", bufs=12))
        wg_pool = stack.enter_context(tc.tile_pool(name="wg_pool", bufs=3))
        wq_pool = stack.enter_context(tc.tile_pool(name="wq_pool", bufs=6))
        bank_pool = stack.enter_context(tc.psum_pool(name="bank_pool", bufs=2))
        acc_pool = stack.enter_context(tc.psum_pool(name="acc_pool", bufs=1))

        warm = keep.tile([P, 1], F32)
        nc.vector.memset(warm[:], 1.0)
        nc.scalar.activation(out=warm[:], in_=warm[:], func=ACT.Abs_reciprocal_sqrt)

        ident = keep.tile([P, P], F32)
        make_identity(nc, ident[:])
        bias_rows = keep.tile([P, P], BF16)
        nc.vector.memset(bias_rows[:], 0.0)
        for row, b in enumerate((b1, b2, b3)):
            nc.scalar.dma_start(out=bias_rows[row : row + 1, :], in_=b.unsqueeze(0))

        perm = keep.tile([P, P], F32)
        nc.vector.tensor_copy(
            out=perm[:].rearrange("i (a n) -> i a n", n=SENTENCES), in_=ident[:].rearrange("i (n a) -> i a n", n=SENTENCES)
        )
        fold_column = keep.tile([P, BLOCK], F32)
        nc.vector.tensor_reduce(
            out=fold_column[:], in_=ident[:].rearrange("i (b n) -> i n b", n=BLOCK), axis=AXIS.X, op=ALU.add
        )
        fold = keep.tile([P, P], F32)
        nc.vector.tensor_copy(
            out=fold[:].rearrange("i (b n) -> i b n", n=BLOCK),
            in_=fold_column[:].unsqueeze(1).to_broadcast([P, P // BLOCK, BLOCK]),
        )
        x_codes = keep.tile([P, PASSES, TOKENS + PAD], U32, align_bytes=64)
        x_scales = keep.tile([P, PASSES, TOKENS + PAD], U8, align_bytes=64)
        x_scales_moved = keep.tile([P, PASSES, TOKENS], U8, align_bytes=64)
        nc.gpsimd.memset(x_codes[:, :, TOKENS:], 0)
        nc.gpsimd.memset(x_scales[:].bitcast(I32), 0)
        code = keep.tile([P, TOKENS], F32, align_bytes=64)
        pooled_cn = keep.tile([P, P], F32)
        nc.gpsimd.memset(pooled_cn[:], 0.0)

        taps = [(width, tap) for width in WIDTHS for tap in range(width)]
        weights = {3: W3, 2: W2, 1: W1}
        x_items = [("x", part * PART_PASSES, PART_PASSES, tt) for part in range(PARTS) for tt in range(TOKEN_TILES)]
        w_items = [("w", part * PART_PASSES, PART_PASSES, i) for part in range(PARTS) for i in range(len(taps))]
        kind, first, passes, i = w_items.pop()
        w_items += [(kind, k, LAST_PASSES, i) for k in range(first, first + passes, LAST_PASSES)]
        x_steps = []
        for item in x_items:
            x_steps += [[item], []] if item[1] > 0 and item[3] == TOKEN_TILES - 1 else [[item]]
        w_steps = [[] for tt in range(TOKEN_TILES - 1)] + [[item] for item in w_items]
        steps = max(len(x_steps), len(w_steps))
        x_steps += [[]] * (steps - len(x_steps))
        load_order = [item for step in range(steps) for item in x_steps[step] + w_steps[step]]
        raw, grouped, x_grouped, banks, w_codes, w_scales = {}, {}, {}, {}, {}, {}

        def load(item):
            kind, first, passes, i = item
            rows = slice(first * K_PASS, (first + passes) * K_PASS)
            if kind == "x":
                raw[item] = x_pool.tile([P, passes * K_PASS], BF16, name="x_raw")
                src = words_emb[:, i * TILE_POSITIONS : (i + 1) * TILE_POSITIONS, rows]
            else:
                width, tap = taps[i]
                raw[item] = w_pool.tile([P, passes, PACK, FEATURES], BF16, name="w_raw")
                src = weights[width][tap, rows, :].rearrange("(g p t) c -> p g t c", p=P, t=PACK)
            nc.sync.dma_start(out=raw[item][:], in_=src)

        for item in load_order[:LOADS_AHEAD]:
            load(item)

        bias = keep.tile([P, len(WIDTHS)], F32)
        peak = keep.tile([P, len(WIDTHS), 2, SENTENCES], F32)
        main, rest = {}, {}

        def transpose_x(item):
            kind, first, passes, tt = item
            if tt == 0:
                x_grouped[first] = xg_pool.tile([P, passes, TOKENS, PACK], BF16, name="x_grouped", align_bytes=64)
            x_words = raw[item][:].bitcast(F32).rearrange("r (g p u) -> r g u p", p=P, u=2)
            for j in range(passes // BANK_PASSES):
                shape = [P, BANK_PASSES, 2, P]
                if first == 0 and tt in (1, 2):
                    bank = acc_pool.tile(shape, F32, name="borrowed", tag=f"{('main', 'rest')[j]}_{tt + 1}")
                else:
                    bank = bank_pool.tile(shape, F32, tag="bank")
                banks[item, j] = bank
                for g in range(BANK_PASSES):
                    for u in range(2):
                        nc.tensor.transpose(bank[:, g, u, :], x_words[:, j * BANK_PASSES + g, u, :], perm[:])

        def copy_x(item):
            kind, first, passes, tt = item
            grouped_words = x_grouped[first][:].rearrange("p g r t -> p (g r t)").bitcast(F32)
            grouped_words = grouped_words.rearrange("p (g r u) -> p g r u", r=TOKENS, u=2)
            for j in range(passes // BANK_PASSES):
                nc.scalar.copy(
                    out=grouped_words[:, j * BANK_PASSES : (j + 1) * BANK_PASSES, tt * P : (tt + 1) * P, :],
                    in_=banks[item, j][:].rearrange("p g u r -> p g r u"),
                )

        def quantise_x(item):
            kind, first, passes, tt = item
            if tt % 2 == 0 and tt < TOKEN_TILES - 1:
                return
            tokens = slice(tt // 2 * 2 * P, (tt + 1) * P)
            for g in range(passes):
                nc.vector.quantize_mx(
                    out=x_codes[:, first + g, tokens].bitcast(FP8X4),
                    scales=x_scales[:, first + g, tokens],
                    in_=x_grouped[first][:, g, tokens, :].rearrange("p r t -> p (r t)"),
                )
            if tt == TOKEN_TILES - 1:
                ks = slice(first, first + passes)
                nc.vector.tensor_copy(
                    out=x_scales_moved[:, ks, :].bitcast(I32), in_=x_scales[:, ks, SENTENCES : SENTENCES + TOKENS].bitcast(I32)
                )

        def regroup(item):
            passes = item[2]
            grouped[item] = wg_pool.tile([P, passes, FEATURES, PACK], BF16, name="w_grouped", align_bytes=64)
            for copy, half in ((nc.vector.tensor_copy, slice(0, passes // 2)), (nc.scalar.copy, slice(passes // 2, passes))):
                copy(
                    out=grouped[item][:, half].rearrange("p g (c i) t -> p g c t i", i=8),
                    in_=raw[item][:, half].rearrange("p g t (c i) -> p g c t i", i=8),
                )

        def quantise_w(item):
            columns = item[2] * FEATURES
            w_codes[item] = wq_pool.tile([P, columns], U32, name="w_codes", align_bytes=64)
            w_scales[item] = wq_pool.tile([P, columns], U8, name="w_scales", align_bytes=64)
            nc.vector.quantize_mx(
                out=w_codes[item][:].bitcast(FP8X4),
                scales=w_scales[item][:],
                in_=grouped[item][:].rearrange("p g c t -> p (g c t)"),
            )

        def multiply(item):
            kind, first, passes, i = item
            width, tap = taps[i]
            if first == 0 and tap == 0:
                main[width] = acc_pool.tile([P, MAIN], F32, name=f"main_{width}")
                rest[width] = acc_pool.tile([P, MAIN], F32, name=f"rest_{width}")
            shift = tap * SENTENCES
            order = [(g, narrow) for g in range(passes) for narrow in (False, True)]
            for g, narrow in sorted(order, key=lambda each: each[1]) if item == w_items[-1] else order:
                k_pass = first + g
                cols = slice(g * FEATURES, (g + 1) * FEATURES)
                if narrow:
                    out, tokens = rest[width][:, 0:REST], slice(shift + MAIN, shift + TOKENS)
                else:
                    out, tokens = main[width][:], slice(shift, shift + MAIN)
                scales = x_scales[:, k_pass, tokens]
                if tap == 1:
                    scales = x_scales_moved[:, k_pass, tokens.start - shift : tokens.stop - shift]
                nc.tensor.matmul_mx(
                    out=out,
                    lhsT=w_codes[item][:, cols].bitcast(FP8X4),
                    lhsT_scale=w_scales[item][:, cols],
                    rhs=x_codes[:, k_pass, tokens].bitcast(FP8X4),
                    rhs_scale=scales,
                    start=(tap == 0 and k_pass == 0),
                    stop=(tap == width - 1 and k_pass == PASSES - 1),
                )

        def own_tokens(width):
            return (POSITIONS - width + 1) * SENTENCES

        def sums(width, lo, hi):
            return main[width][:, lo:hi] if hi <= MAIN else rest[width][:, lo - MAIN : hi - MAIN]

        def bias_of(width):
            return bias[:, WIDTHS.index(width) : WIDTHS.index(width) + 1]

        def raise_code(width, lo, hi):
            nc.vector.scalar_tensor_tensor(
                out=code[:, lo:hi], in0=sums(width, lo, hi), scalar=bias_of(width), in1=code[:, lo:hi], op0=ALU.add, op1=ALU.max
            )

        def take_peak(width):
            for h, (lo, hi) in enumerate(((0, MAIN), (MAIN, own_tokens(width)))):
                by_sentence = sums(width, lo, hi).rearrange("c (p n) -> c n p", n=SENTENCES)
                nc.vector.tensor_reduce(out=peak[:, WIDTHS.index(width), h, :], in_=by_sentence, axis=AXIS.X, op=ALU.max)

        def after_multiply(item):
            kind, first, passes, i = item
            if first + passes < PASSES:
                return
            if taps[i] == (1, 0):
                for lo, hi in ((0, MAIN), (MAIN, TOKENS)):
                    nc.scalar.activation(out=code[:, lo:hi], in_=sums(1, lo, hi), func=ACT.Relu, bias=bias_of(1))
            elif taps[i] == (2, 1):
                raise_code(2, 0, MAIN)
                raise_code(2, MAIN, own_tokens(2))

        loaded = LOADS_AHEAD
        for step in range(steps + MULTIPLY_LAG):
            now_x, now_w = (x_steps[step], w_steps[step]) if step < steps else ([], [])
            last_x = x_steps[step - 1] if 1 <= step <= steps else []
            ready_w, done_w = (w_steps[step - lag] if lag <= step else [] for lag in (MULTIPLY_LAG, MULTIPLY_LAG + 1))
            for item in now_x:
                transpose_x(item)
            if step == 1:
                bias_rows_f32 = keep.tile([P, P], F32)
                nc.vector.tensor_copy(out=bias_rows_f32[:], in_=bias_rows[:])
                bias_bank = bank_pool.tile([P, P], F32, tag="bank")
                nc.tensor.transpose(bias_bank[:], bias_rows_f32[:], ident[:])
                nc.vector.tensor_copy(out=bias[:], in_=bias_bank[:, 0 : len(WIDTHS)])
            for item in ready_w:
                multiply(item)
            for item in now_w:
                regroup(item)
            for item in now_x:
                copy_x(item)
            for item in load_order[loaded : loaded + len(now_x) + len(now_w)]:
                load(item)
            loaded += len(now_x) + len(now_w)
            for item in last_x:
                quantise_x(item)
            for item in now_w:
                quantise_w(item)
            for item in done_w:
                after_multiply(item)

        take_peak(1)

        code_t = keep.tile([P, TOKENS], F32, align_bytes=64)
        squares_t = keep.tile([P, TOKENS], F32)
        part_norm = keep.tile([P, POSITIONS], F32)
        pieces = [slice(0, MAIN // 2), slice(MAIN // 2, MAIN), slice(MAIN, TOKENS)]

        def turn(cols):
            nc.vector.transpose(out=code_t[:, cols], in_=code[:, cols])

        raise_code(3, 0, MAIN // 2)
        raise_code(3, MAIN // 2, MAIN)
        turn(pieces[0])
        raise_code(3, MAIN, own_tokens(3))
        turn(pieces[1])
        turn(pieces[2])
        for cols in pieces:
            nc.scalar.activation(out=squares_t[:, cols], in_=code_t[:, cols], func=ACT.Square)
        for cols in pieces:
            nc.vector.tensor_reduce(
                out=part_norm[:, cols.start // SENTENCES : cols.stop // SENTENCES],
                in_=squares_t[:, cols].rearrange("q (p c) -> q p c", c=BLOCK),
                axis=AXIS.X,
                op=ALU.add,
            )
        norm_bank = bank_pool.tile([P, POSITIONS], F32, tag="bank")
        nc.tensor.matmul(out=norm_bank[:], lhsT=fold[:], rhs=part_norm[:], start=True, stop=True)
        take_peak(2)
        take_peak(3)
        inv_norm = keep.tile([P, POSITIONS], F32)
        nc.scalar.activation(out=inv_norm[:], in_=norm_bank[:], func=ACT.Abs_reciprocal_sqrt)
        top = keep.tile([P, len(WIDTHS), SENTENCES], F32)
        nc.vector.tensor_tensor(out=top[:], in0=peak[:, :, 0, :], in1=peak[:, :, 1, :], op=ALU.max)
        for s, width in enumerate(WIDTHS):
            nc.scalar.activation(out=top[:, s, :], in_=top[:, s, :], func=ACT.Relu, bias=bias_of(width))
        words = keep.tile([P, BLOCK, POSITIONS], F32)
        nc.vector.tensor_scalar_min(inv_norm[:], inv_norm[:], 1.0e12)
        nc.vector.tensor_tensor(
            out=words[:].rearrange("q c (g i) -> q g c i", i=4),
            in0=inv_norm[:].rearrange("q (g i) -> q g i", i=4).unsqueeze(2).to_broadcast([P, POSITIONS // 4, BLOCK, 4]),
            in1=code_t[:].rearrange("q (g i c) -> q g c i", i=4, c=BLOCK),
            op=ALU.mult,
        )
        nc.vector.tensor_reduce(
            out=pooled_cn[:, 0:SENTENCES], in_=top[:].rearrange("c s n -> c n s"), axis=AXIS.X, op=ALU.add
        )
        pooled_bank = bank_pool.tile([P, P], F32, tag="bank")
        nc.tensor.transpose(pooled_bank[:], pooled_cn[:], ident[:])
        pooled_nc = keep.tile([SENTENCES, FEATURES], F32)
        nc.scalar.mul(pooled_nc[:], pooled_bank[0:SENTENCES, :], 1.0 / len(WIDTHS))
        nc.scalar.dma_start(out=out_1[:, :], in_=pooled_nc[:])
        for b in range(P // BLOCK):
            nc.sync.dma_start(
                out=out_0[:, b * BLOCK : (b + 1) * BLOCK, :].rearrange("n c p -> n (c p)"),
                in_=words[b * BLOCK : (b + 1) * BLOCK].rearrange("q c p -> q (c p)"),
            )
